import numpy as np
import ml_dtypes


def mxq(x, axis, fmt="e4m3"):
    dtype, down = {"e4m3": (ml_dtypes.float8_e4m3fn, 7), "e5m2": (ml_dtypes.float8_e5m2, 14)}[fmt]
    v = np.moveaxis(np.asarray(x, np.float32).astype(ml_dtypes.bfloat16).astype(np.float64), axis, -1)
    blocks = v.reshape(v.shape[:-1] + (-1, 32))
    amax = np.abs(blocks).max(-1, keepdims=True)
    byte = np.maximum(np.where(amax > 0, np.frexp(amax)[1] - 1 + 127, 0) - down, 1)
    scale = np.exp2(byte - 127.0)
    codes = (blocks / scale).astype(np.float32).astype(dtype).astype(np.float64)
    return np.moveaxis((codes * scale).reshape(v.shape), -1, axis)


WIDE = False


def mx_kscale(k):
    if not WIDE:
        return np.ones(k)
    levels = np.array([10, -10, 5, -5, 0])
    if k % 512:
        return np.exp2(np.random.permutation(np.resize(levels, k // 32))).repeat(32)
    a = np.empty((k // 512, 16))
    for p in range(k // 512):
        a[p, :8] = np.random.permutation(np.resize(levels, 8))
        for g in range(8):
            far = levels[np.abs(levels - a[p, g]) >= 10]
            a[p, g + 8] = far[np.random.randint(len(far))]
    return np.exp2(a.ravel()).repeat(32)


BF16 = ml_dtypes.bfloat16


def bf(x):
    return np.asarray(x, np.float32).astype(BF16)


def f64(x):
    return np.asarray(x).astype(np.float64)


B, L, E, H, DH, RK, RD, MAXLEN = 4, 1024, 512, 4, 128, 512, 128, 4096


def apply_rope(x, cos, sin):
    cos = cos[None, :, None, :]
    sin = sin[None, :, None, :]
    x1, x2 = x[..., 0::2], x[..., 1::2]
    out_real = x1 * cos - x2 * sin
    out_imag = x1 * sin + x2 * cos
    return np.stack([out_real, out_imag], axis=-1).reshape(x.shape)


def setup_inputs():
    s = mx_kscale(E)
    return {"x": bf(np.random.standard_normal((B, L, E)) * s),
            "cos": bf(np.random.uniform(size=(L, RD // 2))),
            "sin": bf(np.random.uniform(size=(L, RD // 2))),
            "wq": bf(np.random.standard_normal((E, H * (DH + RD))) / np.sqrt(E) / s[:, None])}


def reference(x, cos, sin, wq):
    q_all = (mxq(f64(x), 2, "e4m3") @ mxq(f64(wq), 0, "e4m3")).reshape(B, L, H, DH + RD)
    q_head, q_rope = q_all[..., :DH], q_all[..., DH:]
    q_rope = apply_rope(q_rope, f64(cos), f64(sin))
    return np.concatenate([q_head, q_rope], axis=-1)

@@ -1,0 +1,180 @@
+from contextlib import ExitStack
+
+import concourse.mybir as mybir
+from concourse.masks import make_identity
+
+F32 = mybir.dt.float32
+BF16 = mybir.dt.bfloat16
+U32 = mybir.dt.uint32
+U8 = mybir.dt.uint8
+FP8X4 = mybir.dt.float8_e4m3fn_x4
+ALU = mybir.AluOpType
+
+P = 128
+PACK = 4
+BATCH, SEQ, EMB = 4, 1024, 512
+HEADS, CONTENT, ROPE = 4, 128, 128
+PAIRS = ROPE // 2
+HEAD_COLS = CONTENT + ROPE
+OUT_COLS = HEADS * HEAD_COLS
+BANK = 512
+PLANE = HEADS * PAIRS
+TILES_PER_BATCH = SEQ // P
+STEP_TILES = 2
+STEPS_PER_BATCH = TILES_PER_BATCH // STEP_TILES
+STEPS = BATCH * STEPS_PER_BATCH
+AHEAD = 2
+
+FLOPS = 2 * BATCH * SEQ * EMB * OUT_COLS
+
+
+def tile_multiheadlatentattention_pb_t_kernel(tc, x, cos, sin, wq, out):
+    nc = tc.nc
+    x_view = x.rearrange("b (p t) k -> p b t k", t=TILES_PER_BATCH)
+    out_view = out.rearrange("b (p t) h d -> p b t (h d)", t=TILES_PER_BATCH)
+
+    with ExitStack() as stack:
+        keep = stack.enter_context(tc.tile_pool(name="keep", bufs=1))
+        stage = stack.enter_context(tc.tile_pool(name="stage", bufs=AHEAD + 2))
+        results = stack.enter_context(tc.tile_pool(name="results", bufs=6))
+        psum = stack.enter_context(tc.psum_pool(name="psum", bufs=2))
+
+        x_sb = keep.tile([P, BATCH, TILES_PER_BATCH, EMB], BF16)
+        nc.sync.dma_start(out=x_sb[:, 0, 0:STEP_TILES, :], in_=x_view[:, 0, 0:STEP_TILES, :])
+        w_raw = keep.tile([P, PACK, OUT_COLS], BF16)
+        nc.sync.dma_start(out=w_raw[:], in_=wq.rearrange("(p t) c -> p t c", t=PACK))
+        cos_bf = keep.tile([P, TILES_PER_BATCH, PAIRS], BF16)
+        sin_bf = keep.tile([P, TILES_PER_BATCH, PAIRS], BF16)
+        nc.sync.dma_start(out=cos_bf[:], in_=cos.rearrange("(p t) j -> p t j", t=TILES_PER_BATCH))
+        nc.sync.dma_start(out=sin_bf[:], in_=sin.rearrange("(p t) j -> p t j", t=TILES_PER_BATCH))
+        nc.sync.dma_start(out=x_sb[:, 0, STEP_TILES:, :], in_=x_view[:, 0, STEP_TILES:, :])
+        for b in range(1, BATCH):
+            nc.sync.dma_start(out=x_sb[:, b, :, :], in_=x_view[:, b, :, :])
+
+        identity = keep.tile([P, P], F32)
+        make_identity(nc, identity[:])
+
+        def quantise_x(step):
+            b, t0 = step // STEPS_PER_BATCH, (step % STEPS_PER_BATCH) * STEP_TILES
+            x_words = psum.tile([P, STEP_TILES, 2, P], F32)
+            for i in range(STEP_TILES):
+                for u in range(2):
+                    nc.tensor.transpose(
+                        x_words[:, i, u, :],
+                        x_sb[:, b, t0 + i, :].bitcast(F32)[:, u : 2 * P : 2],
+                        identity[:],
+                    )
+            x_grouped = stage.tile([P, STEP_TILES * P * PACK], BF16, align_bytes=64)
+            nc.scalar.copy(
+                out=x_grouped[:].bitcast(F32).rearrange("p (i r u) -> p i r u", i=STEP_TILES, u=2),
+                in_=x_words[:].rearrange("p i u r -> p i r u"),
+            )
+            x_codes = stage.tile([P, STEP_TILES * P], U32, align_bytes=64)
+            x_scales = stage.tile([P, STEP_TILES * P], U8, align_bytes=64)
+            nc.vector.quantize_mx(
+                out=x_codes[:].bitcast(FP8X4), scales=x_scales[:], in_=x_grouped[:]
+            )
+            return x_codes, x_scales
+
+        quantised = [quantise_x(0)]
+
+        w_grouped = keep.tile([P, OUT_COLS, PACK], BF16, align_bytes=64)
+        w_codes = keep.tile([P, OUT_COLS], U32, align_bytes=64)
+        w_scales = keep.tile([P, OUT_COLS], U8, align_bytes=64)
+        content_cols = slice(0, BANK)
+        rope_cols = slice(BANK, 2 * BANK)
+        b_cols = slice(BANK, BANK + PLANE)
+        a_cols = slice(BANK + PLANE, BANK + 2 * PLANE)
+        w_parts = w_raw[:].rearrange("p t (h x d) -> p t h x d", h=HEADS, x=2)
+        nc.vector.tensor_copy(
+            out=w_grouped[:, content_cols, :].rearrange("p (h d) t -> p h d t", h=HEADS),
+            in_=w_parts[:, :, :, 0, :].rearrange("p t h d -> p h d t"),
+        )
+        w_rope = w_parts[:, :, :, 1, :].rearrange("p t h (j e) -> p t h j e", e=2)
+        for e, cols in ((1, b_cols), (0, a_cols)):
+            nc.scalar.copy(
+                out=w_grouped[:, cols, :].rearrange("p (h j) t -> p h j t", h=HEADS),
+                in_=w_rope[:, :, :, :, e].rearrange("p t h j -> p h j t"),
+            )
+        for cols in (content_cols, rope_cols):
+            nc.vector.quantize_mx(
+                out=w_codes[:, cols].bitcast(FP8X4),
+                scales=w_scales[:, cols],
+                in_=w_grouped[:, cols, :].rearrange("p c t -> p (c t)"),
+            )
+
+        cos_f = keep.tile([P, TILES_PER_BATCH, PAIRS], F32)
+        mixed = keep.tile([P, TILES_PER_BATCH, 2, PAIRS], F32)
+        nc.vector.tensor_copy(out=cos_f[:], in_=cos_bf[:])
+        nc.vector.scalar_tensor_tensor(
+            out=mixed[:, :, 0, :], in0=cos_bf[:], scalar=-1.0, in1=sin_bf[:],
+            op0=ALU.mult, op1=ALU.subtract,
+        )
+        nc.vector.tensor_tensor(out=mixed[:, :, 1, :], in0=sin_bf[:], in1=cos_bf[:], op=ALU.subtract)
+
+        def multiply(sums, x_codes, x_scales, tokens, cols, start, stop):
+            nc.tensor.matmul_mx(
+                out=sums,
+                lhsT=x_codes[:, tokens].bitcast(FP8X4),
+                lhsT_scale=x_scales[:, tokens],
+                rhs=w_codes[:, cols].bitcast(FP8X4),
+                rhs_scale=w_scales[:, cols],
+                start=start,
+                stop=stop,
+            )
+
+        def multiply_and_rotate(step, x_codes, x_scales):
+            b, t0 = step // STEPS_PER_BATCH, (step % STEPS_PER_BATCH) * STEP_TILES
+            ab_ps = psum.tile([P, STEP_TILES, HEADS, PAIRS], F32)
+            for i in range(STEP_TILES):
+                tokens = slice(i * P, (i + 1) * P)
+                group = ab_ps[:, i, :, :].rearrange("p h j -> p (h j)")
+                multiply(group, x_codes, x_scales, tokens, b_cols, True, False)
+                multiply(group, x_codes, x_scales, tokens, a_cols, False, True)
+            shared = results.tile([P, STEP_TILES, HEADS, PAIRS], F32)
+            nc.vector.tensor_tensor(
+                out=shared[:],
+                in0=ab_ps[:],
+                in1=cos_f[:, t0 : t0 + STEP_TILES, :]
+                .unsqueeze(2)
+                .to_broadcast([P, STEP_TILES, HEADS, PAIRS]),
+                op=ALU.mult,
+            )
+            for i in range(STEP_TILES):
+                tokens = slice(i * P, (i + 1) * P)
+                q_sb = results.tile([P, HEADS, HEAD_COLS], F32)
+                content_ps = psum.tile([P, BANK], F32)
+                multiply(content_ps[:], x_codes, x_scales, tokens, content_cols, True, True)
+                nc.scalar.copy(
+                    out=q_sb[:, :, 0:CONTENT],
+                    in_=content_ps[:].rearrange("p (h d) -> p h d", h=HEADS),
+                )
+                rope_ps = psum.tile([P, 2, HEADS, PAIRS], F32)
+                multiply(
+                    rope_ps[:].rearrange("p e h j -> p (e h j)"),
+                    x_codes, x_scales, tokens, rope_cols, True, True,
+                )
+                own = results.tile([P, 2, HEADS, PAIRS], F32)
+                nc.vector.tensor_tensor(
+                    out=own[:],
+                    in0=rope_ps[:],
+                    in1=mixed[:, t0 + i, :, :].unsqueeze(2).to_broadcast([P, 2, HEADS, PAIRS]),
+                    op=ALU.mult,
+                )
+                nc.gpsimd.tensor_tensor(
+                    out=q_sb[:, :, CONTENT:].rearrange("p h (j e) -> p h j e", e=2),
+                    in0=shared[:, i, :, :].unsqueeze(3).to_broadcast([P, HEADS, PAIRS, 2]),
+                    in1=own[:].rearrange("p e h j -> p h j e"),
+                    op=ALU.add,
+                )
+                nc.sync.dma_start(
+                    out=out_view[:, b, t0 + i, :], in_=q_sb[:].rearrange("p h d -> p (h d)")
+                )
+
+        for step in range(1, AHEAD):
+            quantised.append(quantise_x(step))
+        for step in range(STEPS):
+            if step + AHEAD < STEPS:
+                quantised.append(quantise_x(step + AHEAD))
+            x_codes, x_scales = quantised[step]
+            multiply_and_rotate(step, x_codes, x_scales)

@@ -20,10 +20,10 @@ OUT_COLS = HEADS * HEAD_COLS
 BANK = 512
 PLANE = HEADS * PAIRS
 TILES_PER_BATCH = SEQ // P
-STEP_TILES = 2
-STEPS_PER_BATCH = TILES_PER_BATCH // STEP_TILES
-STEPS = BATCH * STEPS_PER_BATCH
-AHEAD = 2
+DUO = 2
+DUOS_PER_BATCH = TILES_PER_BATCH // DUO
+DUOS = BATCH * DUOS_PER_BATCH
+CYCLES = DUOS // 2
 
 FLOPS = 2 * BATCH * SEQ * EMB * OUT_COLS
 
@@ -35,48 +35,60 @@ def tile_multiheadlatentattention_pb_t_kernel(tc, x, cos, sin, wq, out):
 
     with ExitStack() as stack:
         keep = stack.enter_context(tc.tile_pool(name="keep", bufs=1))
-        stage = stack.enter_context(tc.tile_pool(name="stage", bufs=AHEAD + 2))
+        stage = stack.enter_context(tc.tile_pool(name="stage", bufs=4))
+        products = stack.enter_context(tc.tile_pool(name="products", bufs=3))
         results = stack.enter_context(tc.tile_pool(name="results", bufs=6))
         psum = stack.enter_context(tc.psum_pool(name="psum", bufs=2))
+        stack.enter_context(tc.manual_schedule())
 
         x_sb = keep.tile([P, BATCH, TILES_PER_BATCH, EMB], BF16)
-        nc.sync.dma_start(out=x_sb[:, 0, 0:STEP_TILES, :], in_=x_view[:, 0, 0:STEP_TILES, :])
         w_raw = keep.tile([P, PACK, OUT_COLS], BF16)
-        nc.sync.dma_start(out=w_raw[:], in_=wq.rearrange("(p t) c -> p t c", t=PACK))
         cos_bf = keep.tile([P, TILES_PER_BATCH, PAIRS], BF16)
         sin_bf = keep.tile([P, TILES_PER_BATCH, PAIRS], BF16)
+        nc.sync.dma_start(out=x_sb[:, 0, 0:DUO, :], in_=x_view[:, 0, 0:DUO, :])
         nc.sync.dma_start(out=cos_bf[:], in_=cos.rearrange("(p t) j -> p t j", t=TILES_PER_BATCH))
         nc.sync.dma_start(out=sin_bf[:], in_=sin.rearrange("(p t) j -> p t j", t=TILES_PER_BATCH))
-        nc.sync.dma_start(out=x_sb[:, 0, STEP_TILES:, :], in_=x_view[:, 0, STEP_TILES:, :])
+        nc.sync.dma_start(out=w_raw[:], in_=wq.rearrange("(p t) c -> p t c", t=PACK))
+        nc.sync.dma_start(out=x_sb[:, 0, DUO : 2 * DUO, :], in_=x_view[:, 0, DUO : 2 * DUO, :])
+        nc.sync.dma_start(out=x_sb[:, 0, 2 * DUO :, :], in_=x_view[:, 0, 2 * DUO :, :])
         for b in range(1, BATCH):
             nc.sync.dma_start(out=x_sb[:, b, :, :], in_=x_view[:, b, :, :])
 
         identity = keep.tile([P, P], F32)
         make_identity(nc, identity[:])
 
-        def quantise_x(step):
-            b, t0 = step // STEPS_PER_BATCH, (step % STEPS_PER_BATCH) * STEP_TILES
-            x_words = psum.tile([P, STEP_TILES, 2, P], F32)
-            for i in range(STEP_TILES):
+        def place(duo):
+            return duo // DUOS_PER_BATCH, (duo % DUOS_PER_BATCH) * DUO
+
+        x_words_of, x_grouped_of, x_mx_of = {}, {}, {}
+
+        def transpose_x(duo):
+            b, t0 = place(duo)
+            x_words = psum.tile([P, DUO, 2, P], F32)
+            for i in range(DUO):
                 for u in range(2):
                     nc.tensor.transpose(
                         x_words[:, i, u, :],
                         x_sb[:, b, t0 + i, :].bitcast(F32)[:, u : 2 * P : 2],
                         identity[:],
                     )
-            x_grouped = stage.tile([P, STEP_TILES * P * PACK], BF16, align_bytes=64)
-            nc.scalar.copy(
-                out=x_grouped[:].bitcast(F32).rearrange("p (i r u) -> p i r u", i=STEP_TILES, u=2),
-                in_=x_words[:].rearrange("p i u r -> p i r u"),
-            )
-            x_codes = stage.tile([P, STEP_TILES * P], U32, align_bytes=64)
-            x_scales = stage.tile([P, STEP_TILES * P], U8, align_bytes=64)
-            nc.vector.quantize_mx(
-                out=x_codes[:].bitcast(FP8X4), scales=x_scales[:], in_=x_grouped[:]
-            )
-            return x_codes, x_scales
+            x_words_of[duo] = x_words
 
-        quantised = [quantise_x(0)]
+        def regroup_x(duo):
+            x_grouped = stage.tile([P, DUO * P * PACK], BF16, align_bytes=64)
+            nc.scalar.copy(
+                out=x_grouped[:].bitcast(F32).rearrange("p (i r u) -> p i r u", i=DUO, u=2),
+                in_=x_words_of[duo][:].rearrange("p i u r -> p i r u"),
+            )
+            x_grouped_of[duo] = x_grouped
+
+        def quantise_x(duo):
+            x_codes = stage.tile([P, DUO * P], U32, align_bytes=64)
+            x_scales = stage.tile([P, DUO * P], U8, align_bytes=64)
+            nc.vector.quantize_mx(
+                out=x_codes[:].bitcast(FP8X4), scales=x_scales[:], in_=x_grouped_of[duo][:]
+            )
+            x_mx_of[duo] = (x_codes, x_scales)
 
         w_grouped = keep.tile([P, OUT_COLS, PACK], BF16, align_bytes=64)
         w_codes = keep.tile([P, OUT_COLS], U32, align_bytes=64)
@@ -86,17 +98,23 @@ def tile_multiheadlatentattention_pb_t_kernel(tc, x, cos, sin, wq, out):
         b_cols = slice(BANK, BANK + PLANE)
         a_cols = slice(BANK + PLANE, BANK + 2 * PLANE)
         w_parts = w_raw[:].rearrange("p t (h x d) -> p t h x d", h=HEADS, x=2)
-        nc.vector.tensor_copy(
-            out=w_grouped[:, content_cols, :].rearrange("p (h d) t -> p h d t", h=HEADS),
-            in_=w_parts[:, :, :, 0, :].rearrange("p t h d -> p h d t"),
-        )
         w_rope = w_parts[:, :, :, 1, :].rearrange("p t h (j e) -> p t h j e", e=2)
-        for e, cols in ((1, b_cols), (0, a_cols)):
-            nc.scalar.copy(
+
+        def regroup_rope(e, cols):
+            nc.vector.tensor_copy(
                 out=w_grouped[:, cols, :].rearrange("p (h j) t -> p h j t", h=HEADS),
                 in_=w_rope[:, :, :, :, e].rearrange("p t h j -> p h j t"),
             )
-        for cols in (content_cols, rope_cols):
+
+        def regroup_content(h0, h1):
+            nc.scalar.copy(
+                out=w_grouped[:, h0 * CONTENT : h1 * CONTENT, :].rearrange(
+                    "p (h d) t -> p h d t", d=CONTENT
+                ),
+                in_=w_parts[:, :, h0:h1, 0, :].rearrange("p t h d -> p h d t"),
+            )
+
+        def quantise_w(cols):
             nc.vector.quantize_mx(
                 out=w_codes[:, cols].bitcast(FP8X4),
                 scales=w_scales[:, cols],
@@ -105,14 +123,20 @@ def tile_multiheadlatentattention_pb_t_kernel(tc, x, cos, sin, wq, out):
 
         cos_f = keep.tile([P, TILES_PER_BATCH, PAIRS], F32)
         mixed = keep.tile([P, TILES_PER_BATCH, 2, PAIRS], F32)
-        nc.vector.tensor_copy(out=cos_f[:], in_=cos_bf[:])
-        nc.vector.scalar_tensor_tensor(
-            out=mixed[:, :, 0, :], in0=cos_bf[:], scalar=-1.0, in1=sin_bf[:],
-            op0=ALU.mult, op1=ALU.subtract,
-        )
-        nc.vector.tensor_tensor(out=mixed[:, :, 1, :], in0=sin_bf[:], in1=cos_bf[:], op=ALU.subtract)
 
-        def multiply(sums, x_codes, x_scales, tokens, cols, start, stop):
+        def make_tables():
+            nc.scalar.copy(out=cos_f[:], in_=cos_bf[:])
+            nc.vector.scalar_tensor_tensor(
+                out=mixed[:, :, 0, :], in0=cos_bf[:], scalar=-1.0, in1=sin_bf[:],
+                op0=ALU.mult, op1=ALU.subtract,
+            )
+            nc.vector.tensor_tensor(
+                out=mixed[:, :, 1, :], in0=sin_bf[:], in1=cos_bf[:], op=ALU.subtract
+            )
+
+        def multiply(sums, duo, i, cols, start, stop):
+            x_codes, x_scales = x_mx_of[duo]
+            tokens = slice(i * P, (i + 1) * P)
             nc.tensor.matmul_mx(
                 out=sums,
                 lhsT=x_codes[:, tokens].bitcast(FP8X4),
@@ -123,58 +147,114 @@ def tile_multiheadlatentattention_pb_t_kernel(tc, x, cos, sin, wq, out):
                 stop=stop,
             )
 
-        def multiply_and_rotate(step, x_codes, x_scales):
-            b, t0 = step // STEPS_PER_BATCH, (step % STEPS_PER_BATCH) * STEP_TILES
-            ab_ps = psum.tile([P, STEP_TILES, HEADS, PAIRS], F32)
-            for i in range(STEP_TILES):
-                tokens = slice(i * P, (i + 1) * P)
+        shared_of, own_of, q_of = {}, {}, {}
+
+        def shared_product(duo):
+            b, t0 = place(duo)
+            ab_ps = psum.tile([P, DUO, HEADS, PAIRS], F32)
+            for i in range(DUO):
                 group = ab_ps[:, i, :, :].rearrange("p h j -> p (h j)")
-                multiply(group, x_codes, x_scales, tokens, b_cols, True, False)
-                multiply(group, x_codes, x_scales, tokens, a_cols, False, True)
-            shared = results.tile([P, STEP_TILES, HEADS, PAIRS], F32)
+                multiply(group, duo, i, b_cols, True, False)
+                multiply(group, duo, i, a_cols, False, True)
+            shared = products.tile([P, DUO, HEADS, PAIRS], F32)
             nc.vector.tensor_tensor(
                 out=shared[:],
                 in0=ab_ps[:],
-                in1=cos_f[:, t0 : t0 + STEP_TILES, :]
-                .unsqueeze(2)
-                .to_broadcast([P, STEP_TILES, HEADS, PAIRS]),
+                in1=cos_f[:, t0 : t0 + DUO, :].unsqueeze(2).to_broadcast([P, DUO, HEADS, PAIRS]),
                 op=ALU.mult,
             )
-            for i in range(STEP_TILES):
-                tokens = slice(i * P, (i + 1) * P)
-                q_sb = results.tile([P, HEADS, HEAD_COLS], F32)
-                content_ps = psum.tile([P, BANK], F32)
-                multiply(content_ps[:], x_codes, x_scales, tokens, content_cols, True, True)
-                nc.scalar.copy(
-                    out=q_sb[:, :, 0:CONTENT],
-                    in_=content_ps[:].rearrange("p (h d) -> p h d", h=HEADS),
-                )
-                rope_ps = psum.tile([P, 2, HEADS, PAIRS], F32)
-                multiply(
-                    rope_ps[:].rearrange("p e h j -> p (e h j)"),
-                    x_codes, x_scales, tokens, rope_cols, True, True,
-                )
-                own = results.tile([P, 2, HEADS, PAIRS], F32)
-                nc.vector.tensor_tensor(
-                    out=own[:],
-                    in0=rope_ps[:],
-                    in1=mixed[:, t0 + i, :, :].unsqueeze(2).to_broadcast([P, 2, HEADS, PAIRS]),
-                    op=ALU.mult,
-                )
-                nc.gpsimd.tensor_tensor(
-                    out=q_sb[:, :, CONTENT:].rearrange("p h (j e) -> p h j e", e=2),
-                    in0=shared[:, i, :, :].unsqueeze(3).to_broadcast([P, HEADS, PAIRS, 2]),
-                    in1=own[:].rearrange("p e h j -> p h j e"),
-                    op=ALU.add,
-                )
-                nc.sync.dma_start(
-                    out=out_view[:, b, t0 + i, :], in_=q_sb[:].rearrange("p h d -> p (h d)")
-                )
+            shared_of[duo] = shared
+            own = products.tile([P, DUO, 2, HEADS, PAIRS], F32)
+            own_of[duo] = own
+            q_sb = results.tile([P, DUO, HEADS, HEAD_COLS], F32)
+            q_of[duo] = q_sb
 
-        for step in range(1, AHEAD):
-            quantised.append(quantise_x(step))
-        for step in range(STEPS):
-            if step + AHEAD < STEPS:
-                quantised.append(quantise_x(step + AHEAD))
-            x_codes, x_scales = quantised[step]
-            multiply_and_rotate(step, x_codes, x_scales)
+        def own_product(duo, i):
+            b, t0 = place(duo)
+            rope_ps = psum.tile([P, 2, HEADS, PAIRS], F32)
+            multiply(rope_ps[:].rearrange("p e h j -> p (e h j)"), duo, i, rope_cols, True, True)
+            nc.vector.tensor_tensor(
+                out=own_of[duo][:, i, :, :, :],
+                in0=rope_ps[:],
+                in1=mixed[:, t0 + i, :, :].unsqueeze(2).to_broadcast([P, 2, HEADS, PAIRS]),
+                op=ALU.mult,
+            )
+
+        def content(duo, i):
+            content_ps = psum.tile([P, BANK], F32)
+            multiply(content_ps[:], duo, i, content_cols, True, True)
+            nc.scalar.copy(
+                out=q_of[duo][:, i, :, 0:CONTENT],
+                in_=content_ps[:].rearrange("p (h d) -> p h d", h=HEADS),
+            )
+
+        def add(engine, duo, i0, i1):
+            engine.tensor_tensor(
+                out=q_of[duo][:, i0:i1, :, CONTENT:].rearrange("p i h (j e) -> p i h j e", e=2),
+                in0=shared_of[duo][:, i0:i1, :, :]
+                .unsqueeze(4)
+                .to_broadcast([P, i1 - i0, HEADS, PAIRS, 2]),
+                in1=own_of[duo][:, i0:i1, :, :, :].rearrange("p i e h j -> p i h j e"),
+                op=ALU.add,
+            )
+
+        def store(duo, i0, i1):
+            b, t0 = place(duo)
+            nc.sync.dma_start(
+                out=out_view[:, b, t0 + i0 : t0 + i1, :],
+                in_=q_of[duo][:, i0:i1, :, :].rearrange("p i h d -> p i (h d)"),
+            )
+
+        make_tables()
+        transpose_x(0)
+        regroup_x(0)
+        quantise_x(0)
+        regroup_rope(1, b_cols)
+        regroup_rope(0, a_cols)
+        regroup_content(0, 2)
+        transpose_x(1)
+        regroup_x(1)
+        regroup_content(2, 4)
+        quantise_w(b_cols)
+        quantise_w(a_cols)
+        quantise_x(1)
+
+        for cycle in range(CYCLES):
+            mine, theirs = 2 * cycle, 2 * cycle + 1
+            last = cycle == CYCLES - 1
+            if 0 < cycle and not last:
+                regroup_x(mine + 2)
+                regroup_x(theirs + 2)
+            shared_product(mine)
+            for i in range(DUO):
+                own_product(mine, i)
+            if cycle == 0:
+                quantise_w(content_cols)
+                transpose_x(mine + 2)
+                transpose_x(theirs + 2)
+                regroup_x(mine + 2)
+                regroup_x(theirs + 2)
+            for i in range(DUO):
+                content(mine, i)
+            shared_product(theirs)
+            own_product(theirs, 0)
+            content(theirs, 0)
+            if not last:
+                quantise_x(mine + 2)
+                quantise_x(theirs + 2)
+                add(nc.vector, mine, 0, DUO)
+                store(mine, 0, DUO)
+                own_product(theirs, 1)
+                content(theirs, 1)
+                add(nc.gpsimd, theirs, 0, DUO)
+                store(theirs, 0, DUO)
+                if cycle + 2 < CYCLES:
+                    transpose_x(mine + 4)
+                    transpose_x(theirs + 4)
+            else:
+                own_product(theirs, 1)
+                content(theirs, 1)
+                for duo in (mine, theirs):
+                    for i in range(DUO):
+                        add(nc.vector, duo, i, i + 1)
+                        store(duo, i, i + 1)

@@ -48,7 +48,10 @@ def tile_multiheadlatentattention_pb_t_kernel(tc, x, cos, sin, wq, out):
         nc.sync.dma_start(out=x_sb[:, 0, 0:DUO, :], in_=x_view[:, 0, 0:DUO, :])
         nc.sync.dma_start(out=cos_bf[:], in_=cos.rearrange("(p t) j -> p t j", t=TILES_PER_BATCH))
         nc.sync.dma_start(out=sin_bf[:], in_=sin.rearrange("(p t) j -> p t j", t=TILES_PER_BATCH))
-        nc.sync.dma_start(out=w_raw[:], in_=wq.rearrange("(p t) c -> p t c", t=PACK))
+        w_view = wq.rearrange("(p t) c -> p t c", t=PACK)
+        for h0 in (0, 2):
+            cols = slice(h0 * HEAD_COLS, (h0 + 2) * HEAD_COLS)
+            nc.sync.dma_start(out=w_raw[:, :, cols], in_=w_view[:, :, cols])
         nc.sync.dma_start(out=x_sb[:, 0, DUO : 2 * DUO, :], in_=x_view[:, 0, DUO : 2 * DUO, :])
         nc.sync.dma_start(out=x_sb[:, 0, 2 * DUO :, :], in_=x_view[:, 0, 2 * DUO :, :])
         for b in range(1, BATCH):
@@ -100,14 +103,14 @@ def tile_multiheadlatentattention_pb_t_kernel(tc, x, cos, sin, wq, out):
         w_parts = w_raw[:].rearrange("p t (h x d) -> p t h x d", h=HEADS, x=2)
         w_rope = w_parts[:, :, :, 1, :].rearrange("p t h (j e) -> p t h j e", e=2)
 
-        def regroup_rope(e, cols):
-            nc.vector.tensor_copy(
-                out=w_grouped[:, cols, :].rearrange("p (h j) t -> p h j t", h=HEADS),
-                in_=w_rope[:, :, :, :, e].rearrange("p t h j -> p h j t"),
+        def regroup_rope(copy, e, cols, h0, h1):
+            copy(
+                out=w_grouped[:, cols, :].rearrange("p (h j) t -> p h j t", h=HEADS)[:, h0:h1],
+                in_=w_rope[:, :, h0:h1, :, e].rearrange("p t h j -> p h j t"),
             )
 
-        def regroup_content(h0, h1):
-            nc.scalar.copy(
+        def regroup_content(copy, h0, h1):
+            copy(
                 out=w_grouped[:, h0 * CONTENT : h1 * CONTENT, :].rearrange(
                     "p (h d) t -> p h d t", d=CONTENT
                 ),
@@ -147,45 +150,55 @@ def tile_multiheadlatentattention_pb_t_kernel(tc, x, cos, sin, wq, out):
                 stop=stop,
             )
 
+        ab_of, rope_of, content_of = {}, {}, {}
         shared_of, own_of, q_of = {}, {}, {}
 
-        def shared_product(duo):
-            b, t0 = place(duo)
+        def multiply_ab(duo):
             ab_ps = psum.tile([P, DUO, HEADS, PAIRS], F32)
             for i in range(DUO):
                 group = ab_ps[:, i, :, :].rearrange("p h j -> p (h j)")
                 multiply(group, duo, i, b_cols, True, False)
                 multiply(group, duo, i, a_cols, False, True)
+            ab_of[duo] = ab_ps
+
+        def multiply_rope(duo, i):
+            rope_ps = psum.tile([P, 2, HEADS, PAIRS], F32)
+            multiply(rope_ps[:].rearrange("p e h j -> p (e h j)"), duo, i, rope_cols, True, True)
+            rope_of[duo, i] = rope_ps
+
+        def multiply_content(duo, i):
+            content_ps = psum.tile([P, BANK], F32)
+            multiply(content_ps[:], duo, i, content_cols, True, True)
+            content_of[duo, i] = content_ps
+
+        def open_duo(duo):
             shared = products.tile([P, DUO, HEADS, PAIRS], F32)
+            own = products.tile([P, DUO, 2, HEADS, PAIRS], F32)
+            q_sb = results.tile([P, DUO, HEADS, HEAD_COLS], F32)
+            shared_of[duo], own_of[duo], q_of[duo] = shared, own, q_sb
+
+        def shared_product(duo):
+            b, t0 = place(duo)
             nc.vector.tensor_tensor(
-                out=shared[:],
-                in0=ab_ps[:],
+                out=shared_of[duo][:],
+                in0=ab_of[duo][:],
                 in1=cos_f[:, t0 : t0 + DUO, :].unsqueeze(2).to_broadcast([P, DUO, HEADS, PAIRS]),
                 op=ALU.mult,
             )
-            shared_of[duo] = shared
-            own = products.tile([P, DUO, 2, HEADS, PAIRS], F32)
-            own_of[duo] = own
-            q_sb = results.tile([P, DUO, HEADS, HEAD_COLS], F32)
-            q_of[duo] = q_sb
 
         def own_product(duo, i):
             b, t0 = place(duo)
-            rope_ps = psum.tile([P, 2, HEADS, PAIRS], F32)
-            multiply(rope_ps[:].rearrange("p e h j -> p (e h j)"), duo, i, rope_cols, True, True)
             nc.vector.tensor_tensor(
                 out=own_of[duo][:, i, :, :, :],
-                in0=rope_ps[:],
+                in0=rope_of[duo, i][:],
                 in1=mixed[:, t0 + i, :, :].unsqueeze(2).to_broadcast([P, 2, HEADS, PAIRS]),
                 op=ALU.mult,
             )
 
-        def content(duo, i):
-            content_ps = psum.tile([P, BANK], F32)
-            multiply(content_ps[:], duo, i, content_cols, True, True)
+        def copy_content(duo, i):
             nc.scalar.copy(
                 out=q_of[duo][:, i, :, 0:CONTENT],
-                in_=content_ps[:].rearrange("p (h d) -> p h d", h=HEADS),
+                in_=content_of[duo, i][:].rearrange("p (h d) -> p h d", h=HEADS),
             )
 
         def add(engine, duo, i0, i1):
@@ -209,52 +222,82 @@ def tile_multiheadlatentattention_pb_t_kernel(tc, x, cos, sin, wq, out):
         transpose_x(0)
         regroup_x(0)
         quantise_x(0)
-        regroup_rope(1, b_cols)
-        regroup_rope(0, a_cols)
-        regroup_content(0, 2)
+        for h0 in (0, 2):
+            regroup_rope(nc.vector.tensor_copy, 1, b_cols, h0, h0 + 2)
+            regroup_rope(nc.scalar.copy, 0, a_cols, h0, h0 + 2)
         transpose_x(1)
         regroup_x(1)
-        regroup_content(2, 4)
         quantise_w(b_cols)
         quantise_w(a_cols)
-        quantise_x(1)
+        regroup_content(nc.vector.tensor_copy, 0, 2)
+        regroup_content(nc.scalar.copy, 2, 4)
 
         for cycle in range(CYCLES):
             mine, theirs = 2 * cycle, 2 * cycle + 1
-            last = cycle == CYCLES - 1
-            if 0 < cycle and not last:
+            first, last = cycle == 0, cycle == CYCLES - 1
+            gpsimd_helps = cycle < CYCLES - 2
+            open_duo(mine)
+            open_duo(theirs)
+            if not first and not last:
                 regroup_x(mine + 2)
                 regroup_x(theirs + 2)
+            multiply_ab(mine)
             shared_product(mine)
-            for i in range(DUO):
-                own_product(mine, i)
-            if cycle == 0:
+            if first:
+                quantise_x(theirs)
+            multiply_rope(mine, 0)
+            own_product(mine, 0)
+            if first:
+                multiply_rope(mine, 1)
+                own_product(mine, 1)
+                multiply_ab(theirs)
+                multiply_rope(theirs, 0)
                 quantise_w(content_cols)
                 transpose_x(mine + 2)
                 transpose_x(theirs + 2)
                 regroup_x(mine + 2)
+                for i in range(DUO):
+                    multiply_content(mine, i)
+                    copy_content(mine, i)
+                    add(nc.vector, mine, i, i + 1)
+                    store(mine, i, i + 1)
                 regroup_x(theirs + 2)
-            for i in range(DUO):
-                content(mine, i)
+            else:
+                multiply_ab(theirs)
+                multiply_content(mine, 0)
+                copy_content(mine, 0)
+                if last:
+                    add(nc.gpsimd, mine, 0, 1)
+                    store(mine, 0, 1)
+                multiply_rope(mine, 1)
+                own_product(mine, 1)
+                multiply_content(mine, 1)
+                copy_content(mine, 1)
+                multiply_rope(theirs, 0)
             shared_product(theirs)
             own_product(theirs, 0)
-            content(theirs, 0)
+            multiply_content(theirs, 0)
+            copy_content(theirs, 0)
+            multiply_rope(theirs, 1)
+            multiply_content(theirs, 1)
+            copy_content(theirs, 1)
             if not last:
                 quantise_x(mine + 2)
                 quantise_x(theirs + 2)
-                add(nc.vector, mine, 0, DUO)
-                store(mine, 0, DUO)
+            if gpsimd_helps:
+                transpose_x(mine + 4)
+                transpose_x(theirs + 4)
+                if not first:
+                    add(nc.vector, mine, 0, DUO)
+                    store(mine, 0, DUO)
                 own_product(theirs, 1)
-                content(theirs, 1)
                 add(nc.gpsimd, theirs, 0, DUO)
                 store(theirs, 0, DUO)
-                if cycle + 2 < CYCLES:
-                    transpose_x(mine + 4)
-                    transpose_x(theirs + 4)
             else:
+                for i in range(1 if last else 0, DUO):
+                    add(nc.vector, mine, i, i + 1)
+                    store(mine, i, i + 1)
                 own_product(theirs, 1)
-                content(theirs, 1)
-                for duo in (mine, theirs):
-                    for i in range(DUO):
-                        add(nc.vector, duo, i, i + 1)
-                        store(duo, i, i + 1)
+                for i in range(DUO):
+                    add(nc.vector, theirs, i, i + 1)
+                    store(theirs, i, i + 1)

@@ -186,12 +186,12 @@ def tile_multiheadlatentattention_pb_t_kernel(tc, x, cos, sin, wq, out):
                 op=ALU.mult,
             )
 
-        def own_product(duo, i):
+        def own_product(duo, i, h0=0, h1=HEADS):
             b, t0 = place(duo)
             nc.vector.tensor_tensor(
-                out=own_of[duo][:, i, :, :, :],
-                in0=rope_of[duo, i][:],
-                in1=mixed[:, t0 + i, :, :].unsqueeze(2).to_broadcast([P, 2, HEADS, PAIRS]),
+                out=own_of[duo][:, i, :, h0:h1, :],
+                in0=rope_of[duo, i][:, :, h0:h1, :],
+                in1=mixed[:, t0 + i, :, :].unsqueeze(2).to_broadcast([P, 2, h1 - h0, PAIRS]),
                 op=ALU.mult,
             )
 
@@ -281,6 +281,8 @@ def tile_multiheadlatentattention_pb_t_kernel(tc, x, cos, sin, wq, out):
             multiply_rope(theirs, 1)
             multiply_content(theirs, 1)
             copy_content(theirs, 1)
+            if gpsimd_helps:
+                own_product(theirs, 1, 0, HEADS - 1)
             if not last:
                 quantise_x(mine + 2)
                 quantise_x(theirs + 2)
@@ -290,7 +292,7 @@ def tile_multiheadlatentattention_pb_t_kernel(tc, x, cos, sin, wq, out):
                 if not first:
                     add(nc.vector, mine, 0, DUO)
                     store(mine, 0, DUO)
-                own_product(theirs, 1)
+                own_product(theirs, 1, HEADS - 1, HEADS)
                 add(nc.gpsimd, theirs, 0, DUO)
                 store(theirs, 0, DUO)
             else:

@@ -21,9 +21,11 @@ BANK = 512
 PLANE = HEADS * PAIRS
 TILES_PER_BATCH = SEQ // P
 DUO = 2
-DUOS_PER_BATCH = TILES_PER_BATCH // DUO
-DUOS = BATCH * DUOS_PER_BATCH
-CYCLES = DUOS // 2
+CYCLE = 4
+CYCLES_PER_BATCH = TILES_PER_BATCH // CYCLE
+CYCLES = BATCH * CYCLES_PER_BATCH
+UNITS = CYCLE * HEADS
+VECTOR_UNITS = 6
 
 FLOPS = 2 * BATCH * SEQ * EMB * OUT_COLS
 
@@ -35,9 +37,9 @@ def tile_multiheadlatentattention_pb_t_kernel(tc, x, cos, sin, wq, out):
 
     with ExitStack() as stack:
         keep = stack.enter_context(tc.tile_pool(name="keep", bufs=1))
-        stage = stack.enter_context(tc.tile_pool(name="stage", bufs=4))
+        stage = stack.enter_context(tc.tile_pool(name="stage", bufs=3))
         products = stack.enter_context(tc.tile_pool(name="products", bufs=3))
-        results = stack.enter_context(tc.tile_pool(name="results", bufs=6))
+        results = stack.enter_context(tc.tile_pool(name="results", bufs=4))
         psum = stack.enter_context(tc.psum_pool(name="psum", bufs=2))
         stack.enter_context(tc.manual_schedule())
 
@@ -52,46 +54,53 @@ def tile_multiheadlatentattention_pb_t_kernel(tc, x, cos, sin, wq, out):
         for h0 in (0, 2):
             cols = slice(h0 * HEAD_COLS, (h0 + 2) * HEAD_COLS)
             nc.sync.dma_start(out=w_raw[:, :, cols], in_=w_view[:, :, cols])
-        nc.sync.dma_start(out=x_sb[:, 0, DUO : 2 * DUO, :], in_=x_view[:, 0, DUO : 2 * DUO, :])
-        nc.sync.dma_start(out=x_sb[:, 0, 2 * DUO :, :], in_=x_view[:, 0, 2 * DUO :, :])
+        nc.sync.dma_start(out=x_sb[:, 0, DUO:CYCLE, :], in_=x_view[:, 0, DUO:CYCLE, :])
+        nc.sync.dma_start(out=x_sb[:, 0, CYCLE:, :], in_=x_view[:, 0, CYCLE:, :])
         for b in range(1, BATCH):
             nc.sync.dma_start(out=x_sb[:, b, :, :], in_=x_view[:, b, :, :])
 
         identity = keep.tile([P, P], F32)
         make_identity(nc, identity[:])
 
-        def place(duo):
-            return duo // DUOS_PER_BATCH, (duo % DUOS_PER_BATCH) * DUO
+        def place(cycle):
+            return cycle // CYCLES_PER_BATCH, (cycle % CYCLES_PER_BATCH) * CYCLE
 
-        x_words_of, x_grouped_of, x_mx_of = {}, {}, {}
+        x_words_of, x_grouped_of, x_codes_of, x_scales_of = {}, {}, {}, {}
 
-        def transpose_x(duo):
-            b, t0 = place(duo)
+        def open_x(cycle):
+            x_grouped = stage.tile([P, CYCLE * P * PACK], BF16, align_bytes=64)
+            x_codes = stage.tile([P, CYCLE * P], U32, align_bytes=64)
+            x_scales = stage.tile([P, CYCLE * P], U8, align_bytes=64)
+            x_grouped_of[cycle], x_codes_of[cycle], x_scales_of[cycle] = x_grouped, x_codes, x_scales
+
+        def transpose_x(cycle, duo):
+            b, t0 = place(cycle)
             x_words = psum.tile([P, DUO, 2, P], F32)
             for i in range(DUO):
                 for u in range(2):
                     nc.tensor.transpose(
                         x_words[:, i, u, :],
-                        x_sb[:, b, t0 + i, :].bitcast(F32)[:, u : 2 * P : 2],
+                        x_sb[:, b, t0 + DUO * duo + i, :].bitcast(F32)[:, u : 2 * P : 2],
                         identity[:],
                     )
-            x_words_of[duo] = x_words
+            x_words_of[cycle, duo] = x_words
 
-        def regroup_x(duo):
-            x_grouped = stage.tile([P, DUO * P * PACK], BF16, align_bytes=64)
+        def regroup_x(cycle, duo):
+            width = DUO * P * PACK
             nc.scalar.copy(
-                out=x_grouped[:].bitcast(F32).rearrange("p (i r u) -> p i r u", i=DUO, u=2),
-                in_=x_words_of[duo][:].rearrange("p i u r -> p i r u"),
+                out=x_grouped_of[cycle][:, duo * width : (duo + 1) * width]
+                .bitcast(F32)
+                .rearrange("p (i r u) -> p i r u", i=DUO, u=2),
+                in_=x_words_of[cycle, duo][:].rearrange("p i u r -> p i r u"),
             )
-            x_grouped_of[duo] = x_grouped
 
-        def quantise_x(duo):
-            x_codes = stage.tile([P, DUO * P], U32, align_bytes=64)
-            x_scales = stage.tile([P, DUO * P], U8, align_bytes=64)
+        def quantise_x(cycle, i0, i1):
+            tokens = slice(i0 * P, i1 * P)
             nc.vector.quantize_mx(
-                out=x_codes[:].bitcast(FP8X4), scales=x_scales[:], in_=x_grouped_of[duo][:]
+                out=x_codes_of[cycle][:, tokens].bitcast(FP8X4),
+                scales=x_scales_of[cycle][:, tokens],
+                in_=x_grouped_of[cycle][:, i0 * P * PACK : i1 * P * PACK],
             )
-            x_mx_of[duo] = (x_codes, x_scales)
 
         w_grouped = keep.tile([P, OUT_COLS, PACK], BF16, align_bytes=64)
         w_codes = keep.tile([P, OUT_COLS], U32, align_bytes=64)
@@ -137,13 +146,12 @@ def tile_multiheadlatentattention_pb_t_kernel(tc, x, cos, sin, wq, out):
                 out=mixed[:, :, 1, :], in0=sin_bf[:], in1=cos_bf[:], op=ALU.subtract
             )
 
-        def multiply(sums, duo, i, cols, start, stop):
-            x_codes, x_scales = x_mx_of[duo]
+        def multiply(sums, cycle, i, cols, start, stop):
             tokens = slice(i * P, (i + 1) * P)
             nc.tensor.matmul_mx(
                 out=sums,
-                lhsT=x_codes[:, tokens].bitcast(FP8X4),
-                lhsT_scale=x_scales[:, tokens],
+                lhsT=x_codes_of[cycle][:, tokens].bitcast(FP8X4),
+                lhsT_scale=x_scales_of[cycle][:, tokens],
                 rhs=w_codes[:, cols].bitcast(FP8X4),
                 rhs_scale=w_scales[:, cols],
                 start=start,
@@ -153,153 +161,157 @@ def tile_multiheadlatentattention_pb_t_kernel(tc, x, cos, sin, wq, out):
         ab_of, rope_of, content_of = {}, {}, {}
         shared_of, own_of, q_of = {}, {}, {}
 
-        def multiply_ab(duo):
+        def multiply_ab(cycle, duo):
             ab_ps = psum.tile([P, DUO, HEADS, PAIRS], F32)
             for i in range(DUO):
                 group = ab_ps[:, i, :, :].rearrange("p h j -> p (h j)")
-                multiply(group, duo, i, b_cols, True, False)
-                multiply(group, duo, i, a_cols, False, True)
-            ab_of[duo] = ab_ps
+                multiply(group, cycle, DUO * duo + i, b_cols, True, False)
+                multiply(group, cycle, DUO * duo + i, a_cols, False, True)
+            ab_of[cycle, duo] = ab_ps
 
-        def multiply_rope(duo, i):
+        def multiply_rope(cycle, i):
             rope_ps = psum.tile([P, 2, HEADS, PAIRS], F32)
-            multiply(rope_ps[:].rearrange("p e h j -> p (e h j)"), duo, i, rope_cols, True, True)
-            rope_of[duo, i] = rope_ps
+            multiply(rope_ps[:].rearrange("p e h j -> p (e h j)"), cycle, i, rope_cols, True, True)
+            rope_of[cycle, i] = rope_ps
 
-        def multiply_content(duo, i):
+        def multiply_content(cycle, i):
             content_ps = psum.tile([P, BANK], F32)
-            multiply(content_ps[:], duo, i, content_cols, True, True)
-            content_of[duo, i] = content_ps
+            multiply(content_ps[:], cycle, i, content_cols, True, True)
+            content_of[cycle, i] = content_ps
 
-        def open_duo(duo):
-            shared = products.tile([P, DUO, HEADS, PAIRS], F32)
-            own = products.tile([P, DUO, 2, HEADS, PAIRS], F32)
-            q_sb = results.tile([P, DUO, HEADS, HEAD_COLS], F32)
-            shared_of[duo], own_of[duo], q_of[duo] = shared, own, q_sb
+        def open_results(cycle):
+            shared = products.tile([P, CYCLE, HEADS, PAIRS], F32)
+            own = products.tile([P, CYCLE, HEADS, 2, PAIRS], F32)
+            q_sb = results.tile([P, CYCLE, HEADS, HEAD_COLS], F32)
+            shared_of[cycle], own_of[cycle], q_of[cycle] = shared, own, q_sb
 
-        def shared_product(duo):
-            b, t0 = place(duo)
+        def shared_product(cycle, duo):
+            b, t0 = place(cycle)
+            tiles = slice(DUO * duo, DUO * (duo + 1))
             nc.vector.tensor_tensor(
-                out=shared_of[duo][:],
-                in0=ab_of[duo][:],
-                in1=cos_f[:, t0 : t0 + DUO, :].unsqueeze(2).to_broadcast([P, DUO, HEADS, PAIRS]),
+                out=shared_of[cycle][:, tiles, :, :],
+                in0=ab_of[cycle, duo][:],
+                in1=cos_f[:, t0 + DUO * duo : t0 + DUO * (duo + 1), :]
+                .unsqueeze(2)
+                .to_broadcast([P, DUO, HEADS, PAIRS]),
                 op=ALU.mult,
             )
 
-        def own_product(duo, i, h0=0, h1=HEADS):
-            b, t0 = place(duo)
+        def own_product(cycle, i, h0=0, h1=HEADS):
+            b, t0 = place(cycle)
             nc.vector.tensor_tensor(
-                out=own_of[duo][:, i, :, h0:h1, :],
-                in0=rope_of[duo, i][:, :, h0:h1, :],
-                in1=mixed[:, t0 + i, :, :].unsqueeze(2).to_broadcast([P, 2, h1 - h0, PAIRS]),
+                out=own_of[cycle][:, i, h0:h1, :, :],
+                in0=rope_of[cycle, i][:, :, h0:h1, :].rearrange("p e h j -> p h e j"),
+                in1=mixed[:, t0 + i, :, :].unsqueeze(1).to_broadcast([P, h1 - h0, 2, PAIRS]),
                 op=ALU.mult,
             )
 
-        def copy_content(duo, i):
+        def copy_content(cycle, i):
             nc.scalar.copy(
-                out=q_of[duo][:, i, :, 0:CONTENT],
-                in_=content_of[duo, i][:].rearrange("p (h d) -> p h d", h=HEADS),
+                out=q_of[cycle][:, i, :, 0:CONTENT],
+                in_=content_of[cycle, i][:].rearrange("p (h d) -> p h d", h=HEADS),
             )
 
-        def add(engine, duo, i0, i1):
+        def add(engine, cycle, n0, n1):
+            q_units = q_of[cycle][:].rearrange("p i h d -> p (i h) d")
+            shared_units = shared_of[cycle][:].rearrange("p i h j -> p (i h) j")
+            own_units = own_of[cycle][:].rearrange("p i h e j -> p (i h) e j")
             engine.tensor_tensor(
-                out=q_of[duo][:, i0:i1, :, CONTENT:].rearrange("p i h (j e) -> p i h j e", e=2),
-                in0=shared_of[duo][:, i0:i1, :, :]
-                .unsqueeze(4)
-                .to_broadcast([P, i1 - i0, HEADS, PAIRS, 2]),
-                in1=own_of[duo][:, i0:i1, :, :, :].rearrange("p i e h j -> p i h j e"),
+                out=q_units[:, n0:n1, CONTENT:].rearrange("p n (j e) -> p n j e", e=2),
+                in0=shared_units[:, n0:n1, :].unsqueeze(3).to_broadcast([P, n1 - n0, PAIRS, 2]),
+                in1=own_units[:, n0:n1, :, :].rearrange("p n e j -> p n j e"),
                 op=ALU.add,
             )
 
-        def store(duo, i0, i1):
-            b, t0 = place(duo)
+        def store(cycle, i0, i1):
+            b, t0 = place(cycle)
             nc.sync.dma_start(
                 out=out_view[:, b, t0 + i0 : t0 + i1, :],
-                in_=q_of[duo][:, i0:i1, :, :].rearrange("p i h d -> p i (h d)"),
+                in_=q_of[cycle][:, i0:i1, :, :].rearrange("p i h d -> p i (h d)"),
             )
 
         make_tables()
-        transpose_x(0)
-        regroup_x(0)
-        quantise_x(0)
+        open_x(0)
+        transpose_x(0, 0)
+        regroup_x(0, 0)
+        quantise_x(0, 0, DUO)
         for h0 in (0, 2):
             regroup_rope(nc.vector.tensor_copy, 1, b_cols, h0, h0 + 2)
             regroup_rope(nc.scalar.copy, 0, a_cols, h0, h0 + 2)
-        transpose_x(1)
-        regroup_x(1)
+        transpose_x(0, 1)
+        regroup_x(0, 1)
         quantise_w(b_cols)
         quantise_w(a_cols)
         regroup_content(nc.vector.tensor_copy, 0, 2)
         regroup_content(nc.scalar.copy, 2, 4)
 
         for cycle in range(CYCLES):
-            mine, theirs = 2 * cycle, 2 * cycle + 1
             first, last = cycle == 0, cycle == CYCLES - 1
             gpsimd_helps = cycle < CYCLES - 2
-            open_duo(mine)
-            open_duo(theirs)
-            if not first and not last:
-                regroup_x(mine + 2)
-                regroup_x(theirs + 2)
-            multiply_ab(mine)
-            shared_product(mine)
-            if first:
-                quantise_x(theirs)
-            multiply_rope(mine, 0)
-            own_product(mine, 0)
-            if first:
-                multiply_rope(mine, 1)
-                own_product(mine, 1)
-                multiply_ab(theirs)
-                multiply_rope(theirs, 0)
-                quantise_w(content_cols)
-                transpose_x(mine + 2)
-                transpose_x(theirs + 2)
-                regroup_x(mine + 2)
-                for i in range(DUO):
-                    multiply_content(mine, i)
-                    copy_content(mine, i)
-                    add(nc.vector, mine, i, i + 1)
-                    store(mine, i, i + 1)
-                regroup_x(theirs + 2)
-            else:
-                multiply_ab(theirs)
-                multiply_content(mine, 0)
-                copy_content(mine, 0)
-                if last:
-                    add(nc.gpsimd, mine, 0, 1)
-                    store(mine, 0, 1)
-                multiply_rope(mine, 1)
-                own_product(mine, 1)
-                multiply_content(mine, 1)
-                copy_content(mine, 1)
-                multiply_rope(theirs, 0)
-            shared_product(theirs)
-            own_product(theirs, 0)
-            multiply_content(theirs, 0)
-            copy_content(theirs, 0)
-            multiply_rope(theirs, 1)
-            multiply_content(theirs, 1)
-            copy_content(theirs, 1)
-            if gpsimd_helps:
-                own_product(theirs, 1, 0, HEADS - 1)
+            open_results(cycle)
             if not last:
-                quantise_x(mine + 2)
-                quantise_x(theirs + 2)
-            if gpsimd_helps:
-                transpose_x(mine + 4)
-                transpose_x(theirs + 4)
-                if not first:
-                    add(nc.vector, mine, 0, DUO)
-                    store(mine, 0, DUO)
-                own_product(theirs, 1, HEADS - 1, HEADS)
-                add(nc.gpsimd, theirs, 0, DUO)
-                store(theirs, 0, DUO)
-            else:
-                for i in range(1 if last else 0, DUO):
-                    add(nc.vector, mine, i, i + 1)
-                    store(mine, i, i + 1)
-                own_product(theirs, 1)
+                open_x(cycle + 1)
+            if not first and not last:
+                regroup_x(cycle + 1, 0)
+                regroup_x(cycle + 1, 1)
+            multiply_ab(cycle, 0)
+            shared_product(cycle, 0)
+            if first:
+                quantise_x(cycle, DUO, CYCLE)
+            multiply_rope(cycle, 0)
+            own_product(cycle, 0)
+            if first:
+                multiply_rope(cycle, 1)
+                own_product(cycle, 1)
+                multiply_ab(cycle, 1)
+                multiply_rope(cycle, 2)
+                quantise_w(content_cols)
+                transpose_x(cycle + 1, 0)
+                transpose_x(cycle + 1, 1)
+                regroup_x(cycle + 1, 0)
                 for i in range(DUO):
-                    add(nc.vector, theirs, i, i + 1)
-                    store(theirs, i, i + 1)
+                    multiply_content(cycle, i)
+                    copy_content(cycle, i)
+                    add(nc.vector, cycle, HEADS * i, HEADS * (i + 1))
+                    store(cycle, i, i + 1)
+                regroup_x(cycle + 1, 1)
+            else:
+                multiply_ab(cycle, 1)
+                multiply_content(cycle, 0)
+                copy_content(cycle, 0)
+                if last:
+                    add(nc.gpsimd, cycle, 0, HEADS)
+                    store(cycle, 0, 1)
+                multiply_rope(cycle, 1)
+                own_product(cycle, 1)
+                multiply_content(cycle, 1)
+                copy_content(cycle, 1)
+                multiply_rope(cycle, 2)
+            shared_product(cycle, 1)
+            own_product(cycle, 2)
+            multiply_content(cycle, 2)
+            copy_content(cycle, 2)
+            multiply_rope(cycle, 3)
+            multiply_content(cycle, 3)
+            copy_content(cycle, 3)
+            if gpsimd_helps:
+                own_product(cycle, 3, 0, HEADS - 1)
+            if not last:
+                quantise_x(cycle + 1, 0, DUO)
+                quantise_x(cycle + 1, DUO, CYCLE)
+            if gpsimd_helps:
+                transpose_x(cycle + 2, 0)
+                transpose_x(cycle + 2, 1)
+                mine = DUO * HEADS if first else VECTOR_UNITS
+                if not first:
+                    add(nc.vector, cycle, 0, mine)
+                    store(cycle, 0, mine // HEADS)
+                own_product(cycle, 3, HEADS - 1, HEADS)
+                add(nc.gpsimd, cycle, mine, UNITS)
+                store(cycle, mine // HEADS, CYCLE)
+            else:
+                for i in range(1 if last else 0, CYCLE):
+                    if i == CYCLE - 2:
+                        own_product(cycle, 3)
+                    add(nc.vector, cycle, HEADS * i, HEADS * (i + 1))
+                    store(cycle, i, i + 1)

@@ -25,7 +25,7 @@ CYCLE = 4
 CYCLES_PER_BATCH = TILES_PER_BATCH // CYCLE
 CYCLES = BATCH * CYCLES_PER_BATCH
 UNITS = CYCLE * HEADS
-VECTOR_UNITS = 6
+VECTOR_UNITS = 8
 
 FLOPS = 2 * BATCH * SEQ * EMB * OUT_COLS
 
@@ -102,49 +102,47 @@ def tile_multiheadlatentattention_pb_t_kernel(tc, x, cos, sin, wq, out):
                 in_=x_grouped_of[cycle][:, i0 * P * PACK : i1 * P * PACK],
             )
 
-        w_grouped = keep.tile([P, OUT_COLS, PACK], BF16, align_bytes=64)
-        w_codes = keep.tile([P, OUT_COLS], U32, align_bytes=64)
-        w_scales = keep.tile([P, OUT_COLS], U8, align_bytes=64)
+        w_grouped = keep.tile([P, 3 * BANK, PACK], BF16, align_bytes=64)
+        w_codes = keep.tile([P, 3 * BANK], U32, align_bytes=64)
+        w_scales = keep.tile([P, 3 * BANK], U8, align_bytes=64)
         content_cols = slice(0, BANK)
         rope_cols = slice(BANK, 2 * BANK)
-        b_cols = slice(BANK, BANK + PLANE)
-        a_cols = slice(BANK + PLANE, BANK + 2 * PLANE)
+        a_cols = slice(2 * BANK, 2 * BANK + PLANE)
+        b_cols = slice(2 * BANK + PLANE, 3 * BANK)
         w_parts = w_raw[:].rearrange("p t (h x d) -> p t h x d", h=HEADS, x=2)
         w_rope = w_parts[:, :, :, 1, :].rearrange("p t h (j e) -> p t h j e", e=2)
 
-        def regroup_rope(copy, e, cols, h0, h1):
+        def regroup(copy, part, h0, h1):
+            first_col = part * BANK
             copy(
-                out=w_grouped[:, cols, :].rearrange("p (h j) t -> p h j t", h=HEADS)[:, h0:h1],
-                in_=w_rope[:, :, h0:h1, :, e].rearrange("p t h j -> p h j t"),
-            )
-
-        def regroup_content(copy, h0, h1):
-            copy(
-                out=w_grouped[:, h0 * CONTENT : h1 * CONTENT, :].rearrange(
+                out=w_grouped[:, first_col + h0 * CONTENT : first_col + h1 * CONTENT, :].rearrange(
                     "p (h d) t -> p h d t", d=CONTENT
                 ),
-                in_=w_parts[:, :, h0:h1, 0, :].rearrange("p t h d -> p h d t"),
+                in_=w_parts[:, :, h0:h1, part, :].rearrange("p t h d -> p h d t"),
             )
 
-        def quantise_w(cols):
+        def regroup_ab(h0, h1):
+            for e, cols, sign in ((0, a_cols, 1.0), (1, b_cols, -1.0)):
+                nc.scalar.mul(
+                    out=w_grouped[:, cols, :].rearrange("p (h j) t -> p h j t", h=HEADS)[:, h0:h1],
+                    in_=w_rope[:, :, h0:h1, :, e].rearrange("p t h j -> p h j t"),
+                    mul=sign,
+                )
+
+        def quantise_w(c0, c1):
             nc.vector.quantize_mx(
-                out=w_codes[:, cols].bitcast(FP8X4),
-                scales=w_scales[:, cols],
-                in_=w_grouped[:, cols, :].rearrange("p c t -> p (c t)"),
+                out=w_codes[:, c0:c1].bitcast(FP8X4),
+                scales=w_scales[:, c0:c1],
+                in_=w_grouped[:, c0:c1, :].rearrange("p c t -> p (c t)"),
             )
 
-        cos_f = keep.tile([P, TILES_PER_BATCH, PAIRS], F32)
+        sin_f = keep.tile([P, TILES_PER_BATCH, PAIRS], F32)
         mixed = keep.tile([P, TILES_PER_BATCH, 2, PAIRS], F32)
 
         def make_tables():
-            nc.scalar.copy(out=cos_f[:], in_=cos_bf[:])
-            nc.vector.scalar_tensor_tensor(
-                out=mixed[:, :, 0, :], in0=cos_bf[:], scalar=-1.0, in1=sin_bf[:],
-                op0=ALU.mult, op1=ALU.subtract,
-            )
-            nc.vector.tensor_tensor(
-                out=mixed[:, :, 1, :], in0=sin_bf[:], in1=cos_bf[:], op=ALU.subtract
-            )
+            nc.scalar.copy(out=sin_f[:], in_=sin_bf[:])
+            for e, op in ((0, ALU.subtract), (1, ALU.add)):
+                nc.vector.tensor_tensor(out=mixed[:, :, e, :], in0=cos_bf[:], in1=sin_bf[:], op=op)
 
         def multiply(sums, cycle, i, cols, start, stop):
             tokens = slice(i * P, (i + 1) * P)
@@ -165,13 +163,13 @@ def tile_multiheadlatentattention_pb_t_kernel(tc, x, cos, sin, wq, out):
             ab_ps = psum.tile([P, DUO, HEADS, PAIRS], F32)
             for i in range(DUO):
                 group = ab_ps[:, i, :, :].rearrange("p h j -> p (h j)")
-                multiply(group, cycle, DUO * duo + i, b_cols, True, False)
-                multiply(group, cycle, DUO * duo + i, a_cols, False, True)
+                multiply(group, cycle, DUO * duo + i, a_cols, True, False)
+                multiply(group, cycle, DUO * duo + i, b_cols, False, True)
             ab_of[cycle, duo] = ab_ps
 
         def multiply_rope(cycle, i):
-            rope_ps = psum.tile([P, 2, HEADS, PAIRS], F32)
-            multiply(rope_ps[:].rearrange("p e h j -> p (e h j)"), cycle, i, rope_cols, True, True)
+            rope_ps = psum.tile([P, HEADS, PAIRS, 2], F32)
+            multiply(rope_ps[:].rearrange("p h j e -> p (h j e)"), cycle, i, rope_cols, True, True)
             rope_of[cycle, i] = rope_ps
 
         def multiply_content(cycle, i):
@@ -181,7 +179,7 @@ def tile_multiheadlatentattention_pb_t_kernel(tc, x, cos, sin, wq, out):
 
         def open_results(cycle):
             shared = products.tile([P, CYCLE, HEADS, PAIRS], F32)
-            own = products.tile([P, CYCLE, HEADS, 2, PAIRS], F32)
+            own = products.tile([P, CYCLE, HEADS, PAIRS, 2], F32)
             q_sb = results.tile([P, CYCLE, HEADS, HEAD_COLS], F32)
             shared_of[cycle], own_of[cycle], q_of[cycle] = shared, own, q_sb
 
@@ -191,7 +189,7 @@ def tile_multiheadlatentattention_pb_t_kernel(tc, x, cos, sin, wq, out):
             nc.vector.tensor_tensor(
                 out=shared_of[cycle][:, tiles, :, :],
                 in0=ab_of[cycle, duo][:],
-                in1=cos_f[:, t0 + DUO * duo : t0 + DUO * (duo + 1), :]
+                in1=sin_f[:, t0 + DUO * duo : t0 + DUO * (duo + 1), :]
                 .unsqueeze(2)
                 .to_broadcast([P, DUO, HEADS, PAIRS]),
                 op=ALU.mult,
@@ -201,8 +199,11 @@ def tile_multiheadlatentattention_pb_t_kernel(tc, x, cos, sin, wq, out):
             b, t0 = place(cycle)
             nc.vector.tensor_tensor(
                 out=own_of[cycle][:, i, h0:h1, :, :],
-                in0=rope_of[cycle, i][:, :, h0:h1, :].rearrange("p e h j -> p h e j"),
-                in1=mixed[:, t0 + i, :, :].unsqueeze(1).to_broadcast([P, h1 - h0, 2, PAIRS]),
+                in0=rope_of[cycle, i][:, h0:h1, :, :],
+                in1=mixed[:, t0 + i, :, :]
+                .rearrange("p e j -> p j e")
+                .unsqueeze(1)
+                .to_broadcast([P, h1 - h0, PAIRS, 2]),
                 op=ALU.mult,
             )
 
@@ -215,11 +216,11 @@ def tile_multiheadlatentattention_pb_t_kernel(tc, x, cos, sin, wq, out):
         def add(engine, cycle, n0, n1):
             q_units = q_of[cycle][:].rearrange("p i h d -> p (i h) d")
             shared_units = shared_of[cycle][:].rearrange("p i h j -> p (i h) j")
-            own_units = own_of[cycle][:].rearrange("p i h e j -> p (i h) e j")
+            own_units = own_of[cycle][:].rearrange("p i h j e -> p (i h) j e")
             engine.tensor_tensor(
                 out=q_units[:, n0:n1, CONTENT:].rearrange("p n (j e) -> p n j e", e=2),
                 in0=shared_units[:, n0:n1, :].unsqueeze(3).to_broadcast([P, n1 - n0, PAIRS, 2]),
-                in1=own_units[:, n0:n1, :, :].rearrange("p n e j -> p n j e"),
+                in1=own_units[:, n0:n1, :, :],
                 op=ALU.add,
             )
 
@@ -236,14 +237,14 @@ def tile_multiheadlatentattention_pb_t_kernel(tc, x, cos, sin, wq, out):
         regroup_x(0, 0)
         quantise_x(0, 0, DUO)
         for h0 in (0, 2):
-            regroup_rope(nc.vector.tensor_copy, 1, b_cols, h0, h0 + 2)
-            regroup_rope(nc.scalar.copy, 0, a_cols, h0, h0 + 2)
+            regroup(nc.vector.tensor_copy, 1, h0, h0 + 2)
+            regroup_ab(h0, h0 + 2)
         transpose_x(0, 1)
         regroup_x(0, 1)
-        quantise_w(b_cols)
-        quantise_w(a_cols)
-        regroup_content(nc.vector.tensor_copy, 0, 2)
-        regroup_content(nc.scalar.copy, 2, 4)
+        quantise_w(BANK, 2 * BANK)
+        regroup(nc.vector.tensor_copy, 0, 0, 2)
+        quantise_w(2 * BANK, 3 * BANK)
+        regroup(nc.scalar.copy, 0, 2, 4)
 
         for cycle in range(CYCLES):
             first, last = cycle == 0, cycle == CYCLES - 1
@@ -251,31 +252,34 @@ def tile_multiheadlatentattention_pb_t_kernel(tc, x, cos, sin, wq, out):
             open_results(cycle)
             if not last:
                 open_x(cycle + 1)
-            if not first and not last:
-                regroup_x(cycle + 1, 0)
-                regroup_x(cycle + 1, 1)
-            multiply_ab(cycle, 0)
-            shared_product(cycle, 0)
             if first:
-                quantise_x(cycle, DUO, CYCLE)
-            multiply_rope(cycle, 0)
-            own_product(cycle, 0)
-            if first:
+                multiply_rope(cycle, 0)
+                own_product(cycle, 0)
                 multiply_rope(cycle, 1)
                 own_product(cycle, 1)
+                multiply_ab(cycle, 0)
+                quantise_x(cycle, DUO, CYCLE)
+                shared_product(cycle, 0)
+                for duo in range(2):
+                    transpose_x(cycle + 1, duo)
+                    regroup_x(cycle + 1, duo)
                 multiply_ab(cycle, 1)
                 multiply_rope(cycle, 2)
-                quantise_w(content_cols)
-                transpose_x(cycle + 1, 0)
-                transpose_x(cycle + 1, 1)
-                regroup_x(cycle + 1, 0)
+                multiply_rope(cycle, 3)
+                quantise_w(0, BANK)
                 for i in range(DUO):
                     multiply_content(cycle, i)
                     copy_content(cycle, i)
                     add(nc.vector, cycle, HEADS * i, HEADS * (i + 1))
                     store(cycle, i, i + 1)
-                regroup_x(cycle + 1, 1)
             else:
+                if not last:
+                    regroup_x(cycle + 1, 0)
+                    regroup_x(cycle + 1, 1)
+                multiply_ab(cycle, 0)
+                shared_product(cycle, 0)
+                multiply_rope(cycle, 0)
+                own_product(cycle, 0)
                 multiply_ab(cycle, 1)
                 multiply_content(cycle, 0)
                 copy_content(cycle, 0)
@@ -287,21 +291,21 @@ def tile_multiheadlatentattention_pb_t_kernel(tc, x, cos, sin, wq, out):
                 multiply_content(cycle, 1)
                 copy_content(cycle, 1)
                 multiply_rope(cycle, 2)
+                multiply_rope(cycle, 3)
             shared_product(cycle, 1)
             own_product(cycle, 2)
-            multiply_content(cycle, 2)
-            copy_content(cycle, 2)
-            multiply_rope(cycle, 3)
-            multiply_content(cycle, 3)
-            copy_content(cycle, 3)
+            if gpsimd_helps:
+                transpose_x(cycle + 2, 0)
+                transpose_x(cycle + 2, 1)
+            for i in range(DUO, CYCLE):
+                multiply_content(cycle, i)
+                copy_content(cycle, i)
             if gpsimd_helps:
                 own_product(cycle, 3, 0, HEADS - 1)
             if not last:
                 quantise_x(cycle + 1, 0, DUO)
                 quantise_x(cycle + 1, DUO, CYCLE)
             if gpsimd_helps:
-                transpose_x(cycle + 2, 0)
-                transpose_x(cycle + 2, 1)
                 mine = DUO * HEADS if first else VECTOR_UNITS
                 if not first:
                     add(nc.vector, cycle, 0, mine)

@@ -24,8 +24,7 @@ DUO = 2
 CYCLE = 4
 CYCLES_PER_BATCH = TILES_PER_BATCH // CYCLE
 CYCLES = BATCH * CYCLES_PER_BATCH
-UNITS = CYCLE * HEADS
-VECTOR_UNITS = 8
+DUOS = CYCLES * CYCLE // DUO
 
 FLOPS = 2 * BATCH * SEQ * EMB * OUT_COLS
 
@@ -37,7 +36,7 @@ def tile_multiheadlatentattention_pb_t_kernel(tc, x, cos, sin, wq, out):
 
     with ExitStack() as stack:
         keep = stack.enter_context(tc.tile_pool(name="keep", bufs=1))
-        stage = stack.enter_context(tc.tile_pool(name="stage", bufs=3))
+        stage = stack.enter_context(tc.tile_pool(name="stage", bufs=6))
         products = stack.enter_context(tc.tile_pool(name="products", bufs=3))
         results = stack.enter_context(tc.tile_pool(name="results", bufs=4))
         psum = stack.enter_context(tc.psum_pool(name="psum", bufs=2))
@@ -65,42 +64,36 @@ def tile_multiheadlatentattention_pb_t_kernel(tc, x, cos, sin, wq, out):
         def place(cycle):
             return cycle // CYCLES_PER_BATCH, (cycle % CYCLES_PER_BATCH) * CYCLE
 
-        x_words_of, x_grouped_of, x_codes_of, x_scales_of = {}, {}, {}, {}
+        x_words_of, x_grouped_of, x_mx_of = {}, {}, {}
 
-        def open_x(cycle):
-            x_grouped = stage.tile([P, CYCLE * P * PACK], BF16, align_bytes=64)
-            x_codes = stage.tile([P, CYCLE * P], U32, align_bytes=64)
-            x_scales = stage.tile([P, CYCLE * P], U8, align_bytes=64)
-            x_grouped_of[cycle], x_codes_of[cycle], x_scales_of[cycle] = x_grouped, x_codes, x_scales
-
-        def transpose_x(cycle, duo):
-            b, t0 = place(cycle)
+        def transpose_x(duo):
+            b, t0 = place(duo // 2)
+            t0 += DUO * (duo % 2)
             x_words = psum.tile([P, DUO, 2, P], F32)
             for i in range(DUO):
                 for u in range(2):
                     nc.tensor.transpose(
                         x_words[:, i, u, :],
-                        x_sb[:, b, t0 + DUO * duo + i, :].bitcast(F32)[:, u : 2 * P : 2],
+                        x_sb[:, b, t0 + i, :].bitcast(F32)[:, u : 2 * P : 2],
                         identity[:],
                     )
-            x_words_of[cycle, duo] = x_words
+            x_words_of[duo] = x_words
 
-        def regroup_x(cycle, duo):
-            width = DUO * P * PACK
+        def regroup_x(duo):
+            x_grouped = stage.tile([P, DUO * P * PACK], BF16, align_bytes=64)
             nc.scalar.copy(
-                out=x_grouped_of[cycle][:, duo * width : (duo + 1) * width]
-                .bitcast(F32)
-                .rearrange("p (i r u) -> p i r u", i=DUO, u=2),
-                in_=x_words_of[cycle, duo][:].rearrange("p i u r -> p i r u"),
+                out=x_grouped[:].bitcast(F32).rearrange("p (i r u) -> p i r u", i=DUO, u=2),
+                in_=x_words_of[duo][:].rearrange("p i u r -> p i r u"),
             )
+            x_grouped_of[duo] = x_grouped
 
-        def quantise_x(cycle, i0, i1):
-            tokens = slice(i0 * P, i1 * P)
+        def quantise_x(duo):
+            x_codes = stage.tile([P, DUO * P], U32, align_bytes=64)
+            x_scales = stage.tile([P, DUO * P], U8, align_bytes=64)
             nc.vector.quantize_mx(
-                out=x_codes_of[cycle][:, tokens].bitcast(FP8X4),
-                scales=x_scales_of[cycle][:, tokens],
-                in_=x_grouped_of[cycle][:, i0 * P * PACK : i1 * P * PACK],
+                out=x_codes[:].bitcast(FP8X4), scales=x_scales[:], in_=x_grouped_of[duo][:]
             )
+            x_mx_of[duo] = (x_codes, x_scales)
 
         w_grouped = keep.tile([P, 3 * BANK, PACK], BF16, align_bytes=64)
         w_codes = keep.tile([P, 3 * BANK], U32, align_bytes=64)
@@ -145,11 +138,12 @@ def tile_multiheadlatentattention_pb_t_kernel(tc, x, cos, sin, wq, out):
                 nc.vector.tensor_tensor(out=mixed[:, :, e, :], in0=cos_bf[:], in1=sin_bf[:], op=op)
 
         def multiply(sums, cycle, i, cols, start, stop):
-            tokens = slice(i * P, (i + 1) * P)
+            x_codes, x_scales = x_mx_of[(CYCLE * cycle + i) // DUO]
+            tokens = slice((i % DUO) * P, (i % DUO + 1) * P)
             nc.tensor.matmul_mx(
                 out=sums,
-                lhsT=x_codes_of[cycle][:, tokens].bitcast(FP8X4),
-                lhsT_scale=x_scales_of[cycle][:, tokens],
+                lhsT=x_codes[:, tokens].bitcast(FP8X4),
+                lhsT_scale=x_scales[:, tokens],
                 rhs=w_codes[:, cols].bitcast(FP8X4),
                 rhs_scale=w_scales[:, cols],
                 start=start,
@@ -213,14 +207,15 @@ def tile_multiheadlatentattention_pb_t_kernel(tc, x, cos, sin, wq, out):
                 in_=content_of[cycle, i][:].rearrange("p (h d) -> p h d", h=HEADS),
             )
 
-        def add(engine, cycle, n0, n1):
-            q_units = q_of[cycle][:].rearrange("p i h d -> p (i h) d")
-            shared_units = shared_of[cycle][:].rearrange("p i h j -> p (i h) j")
-            own_units = own_of[cycle][:].rearrange("p i h j e -> p (i h) j e")
+        def add(engine, cycle, i0, i1):
+            n0, n1 = i0 * HEADS, i1 * HEADS
+            q_heads = q_of[cycle][:].rearrange("p i h d -> p (i h) d")
+            shared_heads = shared_of[cycle][:].rearrange("p i h j -> p (i h) j")
+            own_heads = own_of[cycle][:].rearrange("p i h j e -> p (i h) j e")
             engine.tensor_tensor(
-                out=q_units[:, n0:n1, CONTENT:].rearrange("p n (j e) -> p n j e", e=2),
-                in0=shared_units[:, n0:n1, :].unsqueeze(3).to_broadcast([P, n1 - n0, PAIRS, 2]),
-                in1=own_units[:, n0:n1, :, :],
+                out=q_heads[:, n0:n1, CONTENT:].rearrange("p n (j e) -> p n j e", e=2),
+                in0=shared_heads[:, n0:n1, :].unsqueeze(3).to_broadcast([P, n1 - n0, PAIRS, 2]),
+                in1=own_heads[:, n0:n1, :, :],
                 op=ALU.add,
             )
 
@@ -232,37 +227,34 @@ def tile_multiheadlatentattention_pb_t_kernel(tc, x, cos, sin, wq, out):
             )
 
         make_tables()
-        open_x(0)
-        transpose_x(0, 0)
-        regroup_x(0, 0)
-        quantise_x(0, 0, DUO)
+        transpose_x(0)
+        regroup_x(0)
+        quantise_x(0)
         for h0 in (0, 2):
             regroup(nc.vector.tensor_copy, 1, h0, h0 + 2)
             regroup_ab(h0, h0 + 2)
-        transpose_x(0, 1)
-        regroup_x(0, 1)
+        transpose_x(1)
+        regroup_x(1)
         quantise_w(BANK, 2 * BANK)
         regroup(nc.vector.tensor_copy, 0, 0, 2)
         quantise_w(2 * BANK, 3 * BANK)
         regroup(nc.scalar.copy, 0, 2, 4)
 
         for cycle in range(CYCLES):
-            first, last = cycle == 0, cycle == CYCLES - 1
-            gpsimd_helps = cycle < CYCLES - 2
+            first = cycle == 0
+            late_tiles = 0 if cycle >= CYCLES - 2 else 2 if cycle == CYCLES - 3 else 3
             open_results(cycle)
-            if not last:
-                open_x(cycle + 1)
             if first:
                 multiply_rope(cycle, 0)
                 own_product(cycle, 0)
                 multiply_rope(cycle, 1)
                 own_product(cycle, 1)
                 multiply_ab(cycle, 0)
-                quantise_x(cycle, DUO, CYCLE)
+                quantise_x(1)
                 shared_product(cycle, 0)
-                for duo in range(2):
-                    transpose_x(cycle + 1, duo)
-                    regroup_x(cycle + 1, duo)
+                for duo in (2, 3):
+                    transpose_x(duo)
+                    regroup_x(duo)
                 multiply_ab(cycle, 1)
                 multiply_rope(cycle, 2)
                 multiply_rope(cycle, 3)
@@ -270,12 +262,11 @@ def tile_multiheadlatentattention_pb_t_kernel(tc, x, cos, sin, wq, out):
                 for i in range(DUO):
                     multiply_content(cycle, i)
                     copy_content(cycle, i)
-                    add(nc.vector, cycle, HEADS * i, HEADS * (i + 1))
-                    store(cycle, i, i + 1)
+                transpose_x(4)
+                regroup_x(4)
+                add(nc.vector, cycle, 0, 1)
+                store(cycle, 0, 1)
             else:
-                if not last:
-                    regroup_x(cycle + 1, 0)
-                    regroup_x(cycle + 1, 1)
                 multiply_ab(cycle, 0)
                 shared_product(cycle, 0)
                 multiply_rope(cycle, 0)
@@ -283,39 +274,36 @@ def tile_multiheadlatentattention_pb_t_kernel(tc, x, cos, sin, wq, out):
                 multiply_ab(cycle, 1)
                 multiply_content(cycle, 0)
                 copy_content(cycle, 0)
-                if last:
-                    add(nc.gpsimd, cycle, 0, HEADS)
+                if late_tiles == 0:
+                    add(nc.gpsimd, cycle, 0, 1)
                     store(cycle, 0, 1)
                 multiply_rope(cycle, 1)
                 own_product(cycle, 1)
                 multiply_content(cycle, 1)
                 copy_content(cycle, 1)
+                for duo in range(2 * cycle + 3, min(2 * cycle + 5, DUOS)):
+                    transpose_x(duo)
+                    regroup_x(duo)
                 multiply_rope(cycle, 2)
                 multiply_rope(cycle, 3)
             shared_product(cycle, 1)
             own_product(cycle, 2)
-            if gpsimd_helps:
-                transpose_x(cycle + 2, 0)
-                transpose_x(cycle + 2, 1)
             for i in range(DUO, CYCLE):
                 multiply_content(cycle, i)
                 copy_content(cycle, i)
-            if gpsimd_helps:
-                own_product(cycle, 3, 0, HEADS - 1)
-            if not last:
-                quantise_x(cycle + 1, 0, DUO)
-                quantise_x(cycle + 1, DUO, CYCLE)
-            if gpsimd_helps:
-                mine = DUO * HEADS if first else VECTOR_UNITS
+            early_heads = HEADS - 1 if late_tiles else HEADS
+            own_product(cycle, 3, 0, early_heads)
+            for duo in range(2 if first else 2 * cycle + 3, min(2 * cycle + 5, DUOS)):
+                quantise_x(duo)
+            if late_tiles:
+                mine = CYCLE - late_tiles
                 if not first:
                     add(nc.vector, cycle, 0, mine)
-                    store(cycle, 0, mine // HEADS)
-                own_product(cycle, 3, HEADS - 1, HEADS)
-                add(nc.gpsimd, cycle, mine, UNITS)
-                store(cycle, mine // HEADS, CYCLE)
+                    store(cycle, 0, mine)
+                own_product(cycle, 3, early_heads, HEADS)
+                add(nc.gpsimd, cycle, mine, CYCLE)
+                store(cycle, mine, CYCLE)
             else:
-                for i in range(1 if last else 0, CYCLE):
-                    if i == CYCLE - 2:
-                        own_product(cycle, 3)
-                    add(nc.vector, cycle, HEADS * i, HEADS * (i + 1))
+                for i in range(1, CYCLE):
+                    add(nc.vector, cycle, i, i + 1)
                     store(cycle, i, i + 1)

@@ -95,32 +95,34 @@ def tile_multiheadlatentattention_pb_t_kernel(tc, x, cos, sin, wq, out):
             )
             x_mx_of[duo] = (x_codes, x_scales)
 
-        w_grouped = keep.tile([P, 3 * BANK, PACK], BF16, align_bytes=64)
-        w_codes = keep.tile([P, 3 * BANK], U32, align_bytes=64)
-        w_scales = keep.tile([P, 3 * BANK], U8, align_bytes=64)
+        w_grouped = keep.tile([P, OUT_COLS, PACK], BF16, align_bytes=64)
+        w_codes = keep.tile([P, OUT_COLS], U32, align_bytes=64)
+        w_scales = keep.tile([P, OUT_COLS], U8, align_bytes=64)
         content_cols = slice(0, BANK)
         rope_cols = slice(BANK, 2 * BANK)
-        a_cols = slice(2 * BANK, 2 * BANK + PLANE)
-        b_cols = slice(2 * BANK + PLANE, 3 * BANK)
+        a_cols = slice(BANK, BANK + PLANE)
+        b_cols = slice(BANK + PLANE, 2 * BANK)
         w_parts = w_raw[:].rearrange("p t (h x d) -> p t h x d", h=HEADS, x=2)
         w_rope = w_parts[:, :, :, 1, :].rearrange("p t h (j e) -> p t h j e", e=2)
 
-        def regroup(copy, part, h0, h1):
-            first_col = part * BANK
+        def regroup_content(copy, h0, h1):
             copy(
-                out=w_grouped[:, first_col + h0 * CONTENT : first_col + h1 * CONTENT, :].rearrange(
+                out=w_grouped[:, h0 * CONTENT : h1 * CONTENT, :].rearrange(
                     "p (h d) t -> p h d t", d=CONTENT
                 ),
-                in_=w_parts[:, :, h0:h1, part, :].rearrange("p t h d -> p h d t"),
+                in_=w_parts[:, :, h0:h1, 0, :].rearrange("p t h d -> p h d t"),
             )
 
-        def regroup_ab(h0, h1):
-            for e, cols, sign in ((0, a_cols, 1.0), (1, b_cols, -1.0)):
-                nc.scalar.mul(
-                    out=w_grouped[:, cols, :].rearrange("p (h j) t -> p h j t", h=HEADS)[:, h0:h1],
-                    in_=w_rope[:, :, h0:h1, :, e].rearrange("p t h j -> p h j t"),
-                    mul=sign,
-                )
+        def regroup_rope(h0, h1):
+            a_grouped, b_grouped = (
+                w_grouped[:, cols, :].rearrange("p (h j) t -> p h j t", h=HEADS)[:, h0:h1]
+                for cols in (a_cols, b_cols)
+            )
+            a_raw, b_raw = (
+                w_rope[:, :, h0:h1, :, e].rearrange("p t h j -> p h j t") for e in (0, 1)
+            )
+            nc.vector.tensor_copy(out=a_grouped, in_=a_raw)
+            nc.scalar.mul(out=b_grouped, in_=b_raw, mul=-1.0)
 
         def quantise_w(c0, c1):
             nc.vector.quantize_mx(
@@ -134,8 +136,13 @@ def tile_multiheadlatentattention_pb_t_kernel(tc, x, cos, sin, wq, out):
 
         def make_tables():
             nc.scalar.copy(out=sin_f[:], in_=sin_bf[:])
-            for e, op in ((0, ALU.subtract), (1, ALU.add)):
-                nc.vector.tensor_tensor(out=mixed[:, :, e, :], in0=cos_bf[:], in1=sin_bf[:], op=op)
+            nc.vector.tensor_tensor(
+                out=mixed[:, :, 0, :], in0=cos_bf[:], in1=sin_bf[:], op=ALU.subtract
+            )
+            nc.vector.scalar_tensor_tensor(
+                out=mixed[:, :, 1, :], in0=cos_bf[:], scalar=-1.0, in1=sin_bf[:],
+                op0=ALU.mult, op1=ALU.subtract,
+            )
 
         def multiply(sums, cycle, i, cols, start, stop):
             x_codes, x_scales = x_mx_of[(CYCLE * cycle + i) // DUO]
@@ -162,8 +169,8 @@ def tile_multiheadlatentattention_pb_t_kernel(tc, x, cos, sin, wq, out):
             ab_of[cycle, duo] = ab_ps
 
         def multiply_rope(cycle, i):
-            rope_ps = psum.tile([P, HEADS, PAIRS, 2], F32)
-            multiply(rope_ps[:].rearrange("p h j e -> p (h j e)"), cycle, i, rope_cols, True, True)
+            rope_ps = psum.tile([P, 2, HEADS, PAIRS], F32)
+            multiply(rope_ps[:].rearrange("p e h j -> p (e h j)"), cycle, i, rope_cols, True, True)
             rope_of[cycle, i] = rope_ps
 
         def multiply_content(cycle, i):
@@ -193,7 +200,7 @@ def tile_multiheadlatentattention_pb_t_kernel(tc, x, cos, sin, wq, out):
             b, t0 = place(cycle)
             nc.vector.tensor_tensor(
                 out=own_of[cycle][:, i, h0:h1, :, :],
-                in0=rope_of[cycle, i][:, h0:h1, :, :],
+                in0=rope_of[cycle, i][:, :, h0:h1, :].rearrange("p e h j -> p h j e"),
                 in1=mixed[:, t0 + i, :, :]
                 .rearrange("p e j -> p j e")
                 .unsqueeze(1)
@@ -231,18 +238,17 @@ def tile_multiheadlatentattention_pb_t_kernel(tc, x, cos, sin, wq, out):
         regroup_x(0)
         quantise_x(0)
         for h0 in (0, 2):
-            regroup(nc.vector.tensor_copy, 1, h0, h0 + 2)
-            regroup_ab(h0, h0 + 2)
+            regroup_rope(h0, h0 + 2)
         transpose_x(1)
         regroup_x(1)
-        quantise_w(BANK, 2 * BANK)
-        regroup(nc.vector.tensor_copy, 0, 0, 2)
-        quantise_w(2 * BANK, 3 * BANK)
-        regroup(nc.scalar.copy, 0, 2, 4)
+        quantise_w(BANK, BANK + PLANE)
+        quantise_w(BANK + PLANE, 2 * BANK)
+        regroup_content(nc.vector.tensor_copy, 0, 2)
+        regroup_content(nc.scalar.copy, 2, 4)
 
         for cycle in range(CYCLES):
-            first = cycle == 0
-            late_tiles = 0 if cycle >= CYCLES - 2 else 2 if cycle == CYCLES - 3 else 3
+            first, last = cycle == 0, cycle == CYCLES - 1
+            late_tiles = 0 if last else 1
             open_results(cycle)
             if first:
                 multiply_rope(cycle, 0)
@@ -274,9 +280,8 @@ def tile_multiheadlatentattention_pb_t_kernel(tc, x, cos, sin, wq, out):
                 multiply_ab(cycle, 1)
                 multiply_content(cycle, 0)
                 copy_content(cycle, 0)
-                if late_tiles == 0:
-                    add(nc.gpsimd, cycle, 0, 1)
-                    store(cycle, 0, 1)
+                add(nc.gpsimd, cycle, 0, 1)
+                store(cycle, 0, 1)
                 multiply_rope(cycle, 1)
                 own_product(cycle, 1)
                 multiply_content(cycle, 1)
@@ -291,19 +296,19 @@ def tile_multiheadlatentattention_pb_t_kernel(tc, x, cos, sin, wq, out):
             for i in range(DUO, CYCLE):
                 multiply_content(cycle, i)
                 copy_content(cycle, i)
+            done = 1
+            if last:
+                add(nc.vector, cycle, 1, 2)
+                store(cycle, 1, 2)
+                done = 2
             early_heads = HEADS - 1 if late_tiles else HEADS
             own_product(cycle, 3, 0, early_heads)
             for duo in range(2 if first else 2 * cycle + 3, min(2 * cycle + 5, DUOS)):
                 quantise_x(duo)
+            for i in range(done, CYCLE - late_tiles):
+                add(nc.vector, cycle, i, i + 1)
+                store(cycle, i, i + 1)
             if late_tiles:
-                mine = CYCLE - late_tiles
-                if not first:
-                    add(nc.vector, cycle, 0, mine)
-                    store(cycle, 0, mine)
                 own_product(cycle, 3, early_heads, HEADS)
-                add(nc.gpsimd, cycle, mine, CYCLE)
-                store(cycle, mine, CYCLE)
-            else:
-                for i in range(1, CYCLE):
-                    add(nc.vector, cycle, i, i + 1)
-                    store(cycle, i, i + 1)
+                add(nc.gpsimd, cycle, 3, CYCLE)
+                store(cycle, 3, CYCLE)

@@ -286,9 +286,6 @@ def tile_multiheadlatentattention_pb_t_kernel(tc, x, cos, sin, wq, out):
                 own_product(cycle, 1)
                 multiply_content(cycle, 1)
                 copy_content(cycle, 1)
-                for duo in range(2 * cycle + 3, min(2 * cycle + 5, DUOS)):
-                    transpose_x(duo)
-                    regroup_x(duo)
                 multiply_rope(cycle, 2)
                 multiply_rope(cycle, 3)
             shared_product(cycle, 1)
@@ -296,6 +293,9 @@ def tile_multiheadlatentattention_pb_t_kernel(tc, x, cos, sin, wq, out):
             for i in range(DUO, CYCLE):
                 multiply_content(cycle, i)
                 copy_content(cycle, i)
+            for duo in range(2 * cycle + 5, min(2 * cycle + 7, DUOS)):
+                transpose_x(duo)
+                regroup_x(duo)
             done = 1
             if last:
                 add(nc.vector, cycle, 1, 2)

@@ -38,7 +38,7 @@ def tile_multiheadlatentattention_pb_t_kernel(tc, x, cos, sin, wq, out):
         keep = stack.enter_context(tc.tile_pool(name="keep", bufs=1))
         stage = stack.enter_context(tc.tile_pool(name="stage", bufs=6))
         products = stack.enter_context(tc.tile_pool(name="products", bufs=3))
-        results = stack.enter_context(tc.tile_pool(name="results", bufs=4))
+        results = stack.enter_context(tc.tile_pool(name="results", bufs=3))
         psum = stack.enter_context(tc.psum_pool(name="psum", bufs=2))
         stack.enter_context(tc.manual_schedule())
 
@@ -158,7 +158,7 @@ def tile_multiheadlatentattention_pb_t_kernel(tc, x, cos, sin, wq, out):
             )
 
         ab_of, rope_of, content_of = {}, {}, {}
-        shared_of, own_of, q_of = {}, {}, {}
+        shared_of, own_of, q_of, q_whole_of = {}, {}, {}, {}
 
         def multiply_ab(cycle, duo):
             ab_ps = psum.tile([P, DUO, HEADS, PAIRS], F32)
@@ -181,8 +181,12 @@ def tile_multiheadlatentattention_pb_t_kernel(tc, x, cos, sin, wq, out):
         def open_results(cycle):
             shared = products.tile([P, CYCLE, HEADS, PAIRS], F32)
             own = products.tile([P, CYCLE, HEADS, PAIRS, 2], F32)
-            q_sb = results.tile([P, CYCLE, HEADS, HEAD_COLS], F32)
-            shared_of[cycle], own_of[cycle], q_of[cycle] = shared, own, q_sb
+            if cycle % CYCLES_PER_BATCH == 0:
+                q_sb = results.tile([P, TILES_PER_BATCH, HEADS, HEAD_COLS], F32)
+                for half in range(CYCLES_PER_BATCH):
+                    q_of[cycle + half] = q_sb[:, half * CYCLE : (half + 1) * CYCLE, :, :]
+                q_whole_of[cycle // CYCLES_PER_BATCH] = q_sb
+            shared_of[cycle], own_of[cycle] = shared, own
 
         def shared_product(cycle, duo):
             b, t0 = place(cycle)
@@ -216,7 +220,7 @@ def tile_multiheadlatentattention_pb_t_kernel(tc, x, cos, sin, wq, out):
 
         def add(engine, cycle, i0, i1):
             n0, n1 = i0 * HEADS, i1 * HEADS
-            q_heads = q_of[cycle][:].rearrange("p i h d -> p (i h) d")
+            q_heads = q_of[cycle].rearrange("p i h d -> p (i h) d")
             shared_heads = shared_of[cycle][:].rearrange("p i h j -> p (i h) j")
             own_heads = own_of[cycle][:].rearrange("p i h j e -> p (i h) j e")
             engine.tensor_tensor(
@@ -228,9 +232,10 @@ def tile_multiheadlatentattention_pb_t_kernel(tc, x, cos, sin, wq, out):
 
         def store(cycle, i0, i1):
             b, t0 = place(cycle)
+            tiles = slice(t0 + i0, t0 + i1)
             nc.sync.dma_start(
-                out=out_view[:, b, t0 + i0 : t0 + i1, :],
-                in_=q_of[cycle][:, i0:i1, :, :].rearrange("p i h d -> p i (h d)"),
+                out=out_view[:, b, tiles, :],
+                in_=q_whole_of[b][:, tiles, :, :].rearrange("p i h d -> p i (h d)"),
             )
 
         make_tables()
@@ -281,7 +286,8 @@ def tile_multiheadlatentattention_pb_t_kernel(tc, x, cos, sin, wq, out):
                 multiply_content(cycle, 0)
                 copy_content(cycle, 0)
                 add(nc.gpsimd, cycle, 0, 1)
-                store(cycle, 0, 1)
+                paired = cycle % CYCLES_PER_BATCH and cycle < CYCLES - CYCLES_PER_BATCH
+                store(cycle, -1 if paired else 0, 1)
                 multiply_rope(cycle, 1)
                 own_product(cycle, 1)
                 multiply_content(cycle, 1)
@@ -307,8 +313,12 @@ def tile_multiheadlatentattention_pb_t_kernel(tc, x, cos, sin, wq, out):
                 quantise_x(duo)
             for i in range(done, CYCLE - late_tiles):
                 add(nc.vector, cycle, i, i + 1)
-                store(cycle, i, i + 1)
+                if cycle >= CYCLES - CYCLES_PER_BATCH:
+                    store(cycle, i, i + 1)
             if late_tiles:
+                if cycle < CYCLES - CYCLES_PER_BATCH:
+                    store(cycle, done, CYCLE - late_tiles)
                 own_product(cycle, 3, early_heads, HEADS)
                 add(nc.gpsimd, cycle, 3, CYCLE)
-                store(cycle, 3, CYCLE)
+                if cycle % CYCLES_PER_BATCH or cycle >= CYCLES - CYCLES_PER_BATCH:
+                    store(cycle, 3, CYCLE)

@@ -36,7 +36,7 @@ def tile_multiheadlatentattention_pb_t_kernel(tc, x, cos, sin, wq, out):
 
     with ExitStack() as stack:
         keep = stack.enter_context(tc.tile_pool(name="keep", bufs=1))
-        stage = stack.enter_context(tc.tile_pool(name="stage", bufs=6))
+        stage = stack.enter_context(tc.tile_pool(name="stage", bufs=5))
         products = stack.enter_context(tc.tile_pool(name="products", bufs=3))
         results = stack.enter_context(tc.tile_pool(name="results", bufs=3))
         psum = stack.enter_context(tc.psum_pool(name="psum", bufs=2))
@@ -49,10 +49,7 @@ def tile_multiheadlatentattention_pb_t_kernel(tc, x, cos, sin, wq, out):
         nc.sync.dma_start(out=x_sb[:, 0, 0:DUO, :], in_=x_view[:, 0, 0:DUO, :])
         nc.sync.dma_start(out=cos_bf[:], in_=cos.rearrange("(p t) j -> p t j", t=TILES_PER_BATCH))
         nc.sync.dma_start(out=sin_bf[:], in_=sin.rearrange("(p t) j -> p t j", t=TILES_PER_BATCH))
-        w_view = wq.rearrange("(p t) c -> p t c", t=PACK)
-        for h0 in (0, 2):
-            cols = slice(h0 * HEAD_COLS, (h0 + 2) * HEAD_COLS)
-            nc.sync.dma_start(out=w_raw[:, :, cols], in_=w_view[:, :, cols])
+        nc.sync.dma_start(out=w_raw[:], in_=wq.rearrange("(p t) c -> p t c", t=PACK))
         nc.sync.dma_start(out=x_sb[:, 0, DUO:CYCLE, :], in_=x_view[:, 0, DUO:CYCLE, :])
         nc.sync.dma_start(out=x_sb[:, 0, CYCLE:, :], in_=x_view[:, 0, CYCLE:, :])
         for b in range(1, BATCH):
@@ -80,20 +77,28 @@ def tile_multiheadlatentattention_pb_t_kernel(tc, x, cos, sin, wq, out):
             x_words_of[duo] = x_words
 
         def regroup_x(duo):
-            x_grouped = stage.tile([P, DUO * P * PACK], BF16, align_bytes=64)
+            if duo < 3 or duo % 2 == 1:
+                x_grouped = stage.tile([P, 2, DUO * P * PACK], BF16, align_bytes=64)
+                x_grouped_of[duo] = x_grouped, 0
+                x_grouped_of[duo + 1] = x_grouped, 1
+            x_grouped, half = x_grouped_of[duo]
             nc.scalar.copy(
-                out=x_grouped[:].bitcast(F32).rearrange("p (i r u) -> p i r u", i=DUO, u=2),
+                out=x_grouped[:, half, :].bitcast(F32).rearrange("p (i r u) -> p i r u", i=DUO, u=2),
                 in_=x_words_of[duo][:].rearrange("p i u r -> p i r u"),
             )
-            x_grouped_of[duo] = x_grouped
 
-        def quantise_x(duo):
-            x_codes = stage.tile([P, DUO * P], U32, align_bytes=64)
-            x_scales = stage.tile([P, DUO * P], U8, align_bytes=64)
+        def quantise_x(duo, duos=1):
+            x_codes = stage.tile([P, 2 * DUO * P], U32, align_bytes=64)
+            x_scales = stage.tile([P, 2 * DUO * P], U8, align_bytes=64)
+            x_grouped, half = x_grouped_of[duo]
+            words = slice(0, duos * DUO * P)
             nc.vector.quantize_mx(
-                out=x_codes[:].bitcast(FP8X4), scales=x_scales[:], in_=x_grouped_of[duo][:]
+                out=x_codes[:, words].bitcast(FP8X4),
+                scales=x_scales[:, words],
+                in_=x_grouped[:, half : half + duos, :].rearrange("p i n -> p (i n)"),
             )
-            x_mx_of[duo] = (x_codes, x_scales)
+            for i in range(duos):
+                x_mx_of[duo + i] = (x_codes, x_scales, i * DUO * P)
 
         w_grouped = keep.tile([P, OUT_COLS, PACK], BF16, align_bytes=64)
         w_codes = keep.tile([P, OUT_COLS], U32, align_bytes=64)
@@ -113,16 +118,12 @@ def tile_multiheadlatentattention_pb_t_kernel(tc, x, cos, sin, wq, out):
                 in_=w_parts[:, :, h0:h1, 0, :].rearrange("p t h d -> p h d t"),
             )
 
-        def regroup_rope(h0, h1):
-            a_grouped, b_grouped = (
-                w_grouped[:, cols, :].rearrange("p (h j) t -> p h j t", h=HEADS)[:, h0:h1]
-                for cols in (a_cols, b_cols)
+        def regroup_rope(e, copy, h0, h1):
+            cols = (a_cols, b_cols)[e]
+            copy(
+                w_grouped[:, cols, :].rearrange("p (h j) t -> p h j t", h=HEADS)[:, h0:h1],
+                w_rope[:, :, h0:h1, :, e].rearrange("p t h j -> p h j t"),
             )
-            a_raw, b_raw = (
-                w_rope[:, :, h0:h1, :, e].rearrange("p t h j -> p h j t") for e in (0, 1)
-            )
-            nc.vector.tensor_copy(out=a_grouped, in_=a_raw)
-            nc.scalar.mul(out=b_grouped, in_=b_raw, mul=-1.0)
 
         def quantise_w(c0, c1):
             nc.vector.quantize_mx(
@@ -145,8 +146,8 @@ def tile_multiheadlatentattention_pb_t_kernel(tc, x, cos, sin, wq, out):
             )
 
         def multiply(sums, cycle, i, cols, start, stop):
-            x_codes, x_scales = x_mx_of[(CYCLE * cycle + i) // DUO]
-            tokens = slice((i % DUO) * P, (i % DUO + 1) * P)
+            x_codes, x_scales, token0 = x_mx_of[(CYCLE * cycle + i) // DUO]
+            tokens = slice(token0 + (i % DUO) * P, token0 + (i % DUO + 1) * P)
             nc.tensor.matmul_mx(
                 out=sums,
                 lhsT=x_codes[:, tokens].bitcast(FP8X4),
@@ -242,8 +243,9 @@ def tile_multiheadlatentattention_pb_t_kernel(tc, x, cos, sin, wq, out):
         transpose_x(0)
         regroup_x(0)
         quantise_x(0)
-        for h0 in (0, 2):
-            regroup_rope(h0, h0 + 2)
+        regroup_rope(1, lambda out, in_: nc.scalar.mul(out, in_, -1.0), 0, HEADS - 1)
+        regroup_rope(0, nc.vector.tensor_copy, 0, HEADS)
+        regroup_rope(1, lambda out, in_: nc.vector.tensor_scalar_mul(out, in_, -1.0), HEADS - 1, HEADS)
         transpose_x(1)
         regroup_x(1)
         quantise_w(BANK, BANK + PLANE)
@@ -309,15 +311,19 @@ def tile_multiheadlatentattention_pb_t_kernel(tc, x, cos, sin, wq, out):
                 done = 2
             early_heads = HEADS - 1 if late_tiles else HEADS
             own_product(cycle, 3, 0, early_heads)
-            for duo in range(2 if first else 2 * cycle + 3, min(2 * cycle + 5, DUOS)):
-                quantise_x(duo)
-            for i in range(done, CYCLE - late_tiles):
-                add(nc.vector, cycle, i, i + 1)
-                if cycle >= CYCLES - CYCLES_PER_BATCH:
+            if first:
+                quantise_x(2)
+            duo = 2 * cycle + 3
+            if duo < DUOS:
+                quantise_x(duo, min(2, DUOS - duo))
+            if cycle < CYCLES - CYCLES_PER_BATCH:
+                add(nc.vector, cycle, done, CYCLE - late_tiles)
+                store(cycle, done, CYCLE - late_tiles)
+            else:
+                for i in range(done, CYCLE - late_tiles):
+                    add(nc.vector, cycle, i, i + 1)
                     store(cycle, i, i + 1)
             if late_tiles:
-                if cycle < CYCLES - CYCLES_PER_BATCH:
-                    store(cycle, done, CYCLE - late_tiles)
                 own_product(cycle, 3, early_heads, HEADS)
                 add(nc.gpsimd, cycle, 3, CYCLE)
                 if cycle % CYCLES_PER_BATCH or cycle >= CYCLES - CYCLES_PER_BATCH:

@@ -24,7 +24,6 @@ DUO = 2
 CYCLE = 4
 CYCLES_PER_BATCH = TILES_PER_BATCH // CYCLE
 CYCLES = BATCH * CYCLES_PER_BATCH
-DUOS = CYCLES * CYCLE // DUO
 
 FLOPS = 2 * BATCH * SEQ * EMB * OUT_COLS
 
@@ -58,47 +57,43 @@ def tile_multiheadlatentattention_pb_t_kernel(tc, x, cos, sin, wq, out):
         identity = keep.tile([P, P], F32)
         make_identity(nc, identity[:])
 
-        def place(cycle):
-            return cycle // CYCLES_PER_BATCH, (cycle % CYCLES_PER_BATCH) * CYCLE
-
-        x_words_of, x_grouped_of, x_mx_of = {}, {}, {}
+        x_words_of, grouped_of, x_mx_of = {}, {}, {}
 
         def transpose_x(duo):
-            b, t0 = place(duo // 2)
-            t0 += DUO * (duo % 2)
             x_words = psum.tile([P, DUO, 2, P], F32)
             for i in range(DUO):
+                b, t = divmod(DUO * duo + i, TILES_PER_BATCH)
                 for u in range(2):
                     nc.tensor.transpose(
                         x_words[:, i, u, :],
-                        x_sb[:, b, t0 + i, :].bitcast(F32)[:, u : 2 * P : 2],
+                        x_sb[:, b, t, :].bitcast(F32)[:, u : 2 * P : 2],
                         identity[:],
                     )
             x_words_of[duo] = x_words
 
-        def regroup_x(duo):
-            if duo < 3 or duo % 2 == 1:
-                x_grouped = stage.tile([P, 2, DUO * P * PACK], BF16, align_bytes=64)
-                x_grouped_of[duo] = x_grouped, 0
-                x_grouped_of[duo + 1] = x_grouped, 1
-            x_grouped, half = x_grouped_of[duo]
+        def regroup_x(cycle, duo):
+            if cycle not in grouped_of:
+                x_grouped = stage.tile([P, CYCLE // DUO, DUO * P * PACK], BF16, align_bytes=64)
+                grouped_of[cycle] = x_grouped
             nc.scalar.copy(
-                out=x_grouped[:, half, :].bitcast(F32).rearrange("p (i r u) -> p i r u", i=DUO, u=2),
-                in_=x_words_of[duo][:].rearrange("p i u r -> p i r u"),
+                out=grouped_of[cycle][:, duo, :]
+                .bitcast(F32)
+                .rearrange("p (i r u) -> p i r u", i=DUO, u=2),
+                in_=x_words_of[CYCLE // DUO * cycle + duo][:].rearrange("p i u r -> p i r u"),
             )
 
-        def quantise_x(duo, duos=1):
-            x_codes = stage.tile([P, 2 * DUO * P], U32, align_bytes=64)
-            x_scales = stage.tile([P, 2 * DUO * P], U8, align_bytes=64)
-            x_grouped, half = x_grouped_of[duo]
-            words = slice(0, duos * DUO * P)
+        def quantise_x(cycle, duo0=0, duo1=CYCLE // DUO):
+            if cycle not in x_mx_of:
+                x_codes = stage.tile([P, CYCLE * P], U32, align_bytes=64)
+                x_scales = stage.tile([P, CYCLE * P], U8, align_bytes=64)
+                x_mx_of[cycle] = (x_codes, x_scales)
+            x_codes, x_scales = x_mx_of[cycle]
+            tokens = slice(duo0 * DUO * P, duo1 * DUO * P)
             nc.vector.quantize_mx(
-                out=x_codes[:, words].bitcast(FP8X4),
-                scales=x_scales[:, words],
-                in_=x_grouped[:, half : half + duos, :].rearrange("p i n -> p (i n)"),
+                out=x_codes[:, tokens].bitcast(FP8X4),
+                scales=x_scales[:, tokens],
+                in_=grouped_of[cycle][:, duo0:duo1, :].rearrange("p i n -> p (i n)"),
             )
-            for i in range(duos):
-                x_mx_of[duo + i] = (x_codes, x_scales, i * DUO * P)
 
         w_grouped = keep.tile([P, OUT_COLS, PACK], BF16, align_bytes=64)
         w_codes = keep.tile([P, OUT_COLS], U32, align_bytes=64)
@@ -145,9 +140,10 @@ def tile_multiheadlatentattention_pb_t_kernel(tc, x, cos, sin, wq, out):
                 op0=ALU.mult, op1=ALU.subtract,
             )
 
-        def multiply(sums, cycle, i, cols, start, stop):
-            x_codes, x_scales, token0 = x_mx_of[(CYCLE * cycle + i) // DUO]
-            tokens = slice(token0 + (i % DUO) * P, token0 + (i % DUO + 1) * P)
+        def multiply(sums, tile, cols, start, stop):
+            cycle, i = divmod(tile, CYCLE)
+            x_codes, x_scales = x_mx_of[cycle]
+            tokens = slice(i * P, (i + 1) * P)
             nc.tensor.matmul_mx(
                 out=sums,
                 lhsT=x_codes[:, tokens].bitcast(FP8X4),
@@ -158,173 +154,169 @@ def tile_multiheadlatentattention_pb_t_kernel(tc, x, cos, sin, wq, out):
                 stop=stop,
             )
 
-        ab_of, rope_of, content_of = {}, {}, {}
-        shared_of, own_of, q_of, q_whole_of = {}, {}, {}, {}
+        ab_of, rope_of, content_of, cycle_of, q_of = {}, {}, {}, {}, {}
 
-        def multiply_ab(cycle, duo):
+        def multiply_ab(duo):
             ab_ps = psum.tile([P, DUO, HEADS, PAIRS], F32)
             for i in range(DUO):
                 group = ab_ps[:, i, :, :].rearrange("p h j -> p (h j)")
-                multiply(group, cycle, DUO * duo + i, a_cols, True, False)
-                multiply(group, cycle, DUO * duo + i, b_cols, False, True)
-            ab_of[cycle, duo] = ab_ps
+                multiply(group, DUO * duo + i, a_cols, True, False)
+                multiply(group, DUO * duo + i, b_cols, False, True)
+            ab_of[duo] = ab_ps
 
-        def multiply_rope(cycle, i):
+        def multiply_rope(tile):
             rope_ps = psum.tile([P, 2, HEADS, PAIRS], F32)
-            multiply(rope_ps[:].rearrange("p e h j -> p (e h j)"), cycle, i, rope_cols, True, True)
-            rope_of[cycle, i] = rope_ps
+            multiply(rope_ps[:].rearrange("p e h j -> p (e h j)"), tile, rope_cols, True, True)
+            rope_of[tile] = rope_ps
 
-        def multiply_content(cycle, i):
+        def multiply_content(tile):
             content_ps = psum.tile([P, BANK], F32)
-            multiply(content_ps[:], cycle, i, content_cols, True, True)
-            content_of[cycle, i] = content_ps
+            multiply(content_ps[:], tile, content_cols, True, True)
+            content_of[tile] = content_ps
 
-        def open_results(cycle):
+        def open_cycle(cycle):
             shared = products.tile([P, CYCLE, HEADS, PAIRS], F32)
             own = products.tile([P, CYCLE, HEADS, PAIRS, 2], F32)
-            if cycle % CYCLES_PER_BATCH == 0:
+            batch, half = divmod(cycle, CYCLES_PER_BATCH)
+            if half == 0:
                 q_sb = results.tile([P, TILES_PER_BATCH, HEADS, HEAD_COLS], F32)
-                for half in range(CYCLES_PER_BATCH):
-                    q_of[cycle + half] = q_sb[:, half * CYCLE : (half + 1) * CYCLE, :, :]
-                q_whole_of[cycle // CYCLES_PER_BATCH] = q_sb
-            shared_of[cycle], own_of[cycle] = shared, own
+                q_of[batch] = q_sb
+            cycle_of[cycle] = (shared, own, q_of[batch][:, half * CYCLE : (half + 1) * CYCLE, :, :])
 
-        def shared_product(cycle, duo):
-            b, t0 = place(cycle)
-            tiles = slice(DUO * duo, DUO * (duo + 1))
+        def shared_product(duo):
+            cycle, i = divmod(DUO * duo, CYCLE)
+            t0 = DUO * duo % TILES_PER_BATCH
             nc.vector.tensor_tensor(
-                out=shared_of[cycle][:, tiles, :, :],
-                in0=ab_of[cycle, duo][:],
-                in1=sin_f[:, t0 + DUO * duo : t0 + DUO * (duo + 1), :]
-                .unsqueeze(2)
-                .to_broadcast([P, DUO, HEADS, PAIRS]),
+                out=cycle_of[cycle][0][:, i : i + DUO, :, :],
+                in0=ab_of[duo][:],
+                in1=sin_f[:, t0 : t0 + DUO, :].unsqueeze(2).to_broadcast([P, DUO, HEADS, PAIRS]),
                 op=ALU.mult,
             )
 
-        def own_product(cycle, i, h0=0, h1=HEADS):
-            b, t0 = place(cycle)
+        def own_product(tile, h0=0, h1=HEADS):
+            cycle, i = divmod(tile, CYCLE)
             nc.vector.tensor_tensor(
-                out=own_of[cycle][:, i, h0:h1, :, :],
-                in0=rope_of[cycle, i][:, :, h0:h1, :].rearrange("p e h j -> p h j e"),
-                in1=mixed[:, t0 + i, :, :]
+                out=cycle_of[cycle][1][:, i, h0:h1, :, :],
+                in0=rope_of[tile][:, :, h0:h1, :].rearrange("p e h j -> p h j e"),
+                in1=mixed[:, tile % TILES_PER_BATCH, :, :]
                 .rearrange("p e j -> p j e")
                 .unsqueeze(1)
                 .to_broadcast([P, h1 - h0, PAIRS, 2]),
                 op=ALU.mult,
             )
 
-        def copy_content(cycle, i):
+        def copy_content(tile):
+            cycle, i = divmod(tile, CYCLE)
             nc.scalar.copy(
-                out=q_of[cycle][:, i, :, 0:CONTENT],
-                in_=content_of[cycle, i][:].rearrange("p (h d) -> p h d", h=HEADS),
+                out=cycle_of[cycle][2][:, i, :, 0:CONTENT],
+                in_=content_of[tile][:].rearrange("p (h d) -> p h d", h=HEADS),
             )
 
-        def add(engine, cycle, i0, i1):
-            n0, n1 = i0 * HEADS, i1 * HEADS
-            q_heads = q_of[cycle].rearrange("p i h d -> p (i h) d")
-            shared_heads = shared_of[cycle][:].rearrange("p i h j -> p (i h) j")
-            own_heads = own_of[cycle][:].rearrange("p i h j e -> p (i h) j e")
+        def add(engine, cycle, n0, n1):
+            shared, own, q_sb = cycle_of[cycle]
             engine.tensor_tensor(
-                out=q_heads[:, n0:n1, CONTENT:].rearrange("p n (j e) -> p n j e", e=2),
-                in0=shared_heads[:, n0:n1, :].unsqueeze(3).to_broadcast([P, n1 - n0, PAIRS, 2]),
-                in1=own_heads[:, n0:n1, :, :],
+                out=q_sb.rearrange("p i h d -> p (i h) d")[:, n0:n1, CONTENT:]
+                .rearrange("p n (j e) -> p n j e", e=2),
+                in0=shared[:]
+                .rearrange("p i h j -> p (i h) j")[:, n0:n1, :]
+                .unsqueeze(3)
+                .to_broadcast([P, n1 - n0, PAIRS, 2]),
+                in1=own[:].rearrange("p i h j e -> p (i h) j e")[:, n0:n1, :, :],
                 op=ALU.add,
             )
 
-        def store(cycle, i0, i1):
-            b, t0 = place(cycle)
-            tiles = slice(t0 + i0, t0 + i1)
+        def store(tile0, tile1):
+            b, t0 = divmod(tile0, TILES_PER_BATCH)
+            tiles = slice(t0, t0 + tile1 - tile0)
             nc.sync.dma_start(
                 out=out_view[:, b, tiles, :],
-                in_=q_whole_of[b][:, tiles, :, :].rearrange("p i h d -> p i (h d)"),
+                in_=q_of[b][:, tiles, :, :].rearrange("p i h d -> p i (h d)"),
             )
 
         make_tables()
         transpose_x(0)
-        regroup_x(0)
-        quantise_x(0)
+        regroup_x(0, 0)
+        quantise_x(0, 0, 1)
         regroup_rope(1, lambda out, in_: nc.scalar.mul(out, in_, -1.0), 0, HEADS - 1)
         regroup_rope(0, nc.vector.tensor_copy, 0, HEADS)
         regroup_rope(1, lambda out, in_: nc.vector.tensor_scalar_mul(out, in_, -1.0), HEADS - 1, HEADS)
         transpose_x(1)
-        regroup_x(1)
+        regroup_x(0, 1)
         quantise_w(BANK, BANK + PLANE)
         quantise_w(BANK + PLANE, 2 * BANK)
         regroup_content(nc.vector.tensor_copy, 0, 2)
         regroup_content(nc.scalar.copy, 2, 4)
+        open_cycle(0)
+        multiply_rope(0)
+        multiply_rope(1)
+        own_product(0)
+        own_product(1)
+        for duo in range(CYCLE // DUO):
+            transpose_x(CYCLE // DUO + duo)
+            regroup_x(1, duo)
+        multiply_ab(0)
+        quantise_x(0, 1, 2)
+        quantise_w(0, BANK)
+        shared_product(0)
+        multiply_ab(1)
+        multiply_rope(2)
+        multiply_rope(3)
+
+        def transpose_ahead(cycle):
+            if cycle + 2 < CYCLES:
+                for duo in range(CYCLE // DUO):
+                    transpose_x(CYCLE // DUO * (cycle + 2) + duo)
+                    regroup_x(cycle + 2, duo)
 
         for cycle in range(CYCLES):
             first, last = cycle == 0, cycle == CYCLES - 1
-            late_tiles = 0 if last else 1
-            open_results(cycle)
-            if first:
-                multiply_rope(cycle, 0)
-                own_product(cycle, 0)
-                multiply_rope(cycle, 1)
-                own_product(cycle, 1)
-                multiply_ab(cycle, 0)
-                quantise_x(1)
-                shared_product(cycle, 0)
-                for duo in (2, 3):
-                    transpose_x(duo)
-                    regroup_x(duo)
-                multiply_ab(cycle, 1)
-                multiply_rope(cycle, 2)
-                multiply_rope(cycle, 3)
-                quantise_w(0, BANK)
-                for i in range(DUO):
-                    multiply_content(cycle, i)
-                    copy_content(cycle, i)
-                transpose_x(4)
-                regroup_x(4)
-                add(nc.vector, cycle, 0, 1)
-                store(cycle, 0, 1)
+            ending = cycle >= CYCLES - CYCLES_PER_BATCH
+            tile0, duo0 = CYCLE * cycle, CYCLE // DUO * cycle
+            if not first:
+                open_cycle(cycle)
+                shared_product(duo0)
+                own_product(tile0)
+                multiply_ab(duo0 + 1)
+            multiply_content(tile0)
+            copy_content(tile0)
+            add(nc.gpsimd, cycle, 0, HEADS)
+            if cycle % CYCLES_PER_BATCH and not ending:
+                store(tile0 - 1, tile0 + 1)
             else:
-                multiply_ab(cycle, 0)
-                shared_product(cycle, 0)
-                multiply_rope(cycle, 0)
-                own_product(cycle, 0)
-                multiply_ab(cycle, 1)
-                multiply_content(cycle, 0)
-                copy_content(cycle, 0)
-                add(nc.gpsimd, cycle, 0, 1)
-                paired = cycle % CYCLES_PER_BATCH and cycle < CYCLES - CYCLES_PER_BATCH
-                store(cycle, -1 if paired else 0, 1)
-                multiply_rope(cycle, 1)
-                own_product(cycle, 1)
-                multiply_content(cycle, 1)
-                copy_content(cycle, 1)
-                multiply_rope(cycle, 2)
-                multiply_rope(cycle, 3)
-            shared_product(cycle, 1)
-            own_product(cycle, 2)
-            for i in range(DUO, CYCLE):
-                multiply_content(cycle, i)
-                copy_content(cycle, i)
-            for duo in range(2 * cycle + 5, min(2 * cycle + 7, DUOS)):
-                transpose_x(duo)
-                regroup_x(duo)
-            done = 1
+                store(tile0, tile0 + 1)
+            if not first:
+                own_product(tile0 + 1)
+            multiply_content(tile0 + 1)
+            copy_content(tile0 + 1)
+            if first:
+                transpose_ahead(cycle)
+            else:
+                multiply_rope(tile0 + 2)
+                multiply_rope(tile0 + 3)
+            shared_product(duo0 + 1)
+            own_product(tile0 + 2)
+            for tile in range(tile0 + 2, tile0 + CYCLE):
+                multiply_content(tile)
+                copy_content(tile)
+            if not first:
+                transpose_ahead(cycle)
+            if ending:
+                add(nc.vector, cycle, HEADS, 2 * HEADS)
+                store(tile0 + 1, tile0 + 2)
             if last:
-                add(nc.vector, cycle, 1, 2)
-                store(cycle, 1, 2)
-                done = 2
-            early_heads = HEADS - 1 if late_tiles else HEADS
-            own_product(cycle, 3, 0, early_heads)
-            if first:
-                quantise_x(2)
-            duo = 2 * cycle + 3
-            if duo < DUOS:
-                quantise_x(duo, min(2, DUOS - duo))
-            if cycle < CYCLES - CYCLES_PER_BATCH:
-                add(nc.vector, cycle, done, CYCLE - late_tiles)
-                store(cycle, done, CYCLE - late_tiles)
+                own_product(tile0 + 3)
+                for n in (2, 3):
+                    add(nc.vector, cycle, n * HEADS, (n + 1) * HEADS)
+                    store(tile0 + n, tile0 + n + 1)
             else:
-                for i in range(done, CYCLE - late_tiles):
-                    add(nc.vector, cycle, i, i + 1)
-                    store(cycle, i, i + 1)
-            if late_tiles:
-                own_product(cycle, 3, early_heads, HEADS)
-                add(nc.gpsimd, cycle, 3, CYCLE)
-                if cycle % CYCLES_PER_BATCH or cycle >= CYCLES - CYCLES_PER_BATCH:
-                    store(cycle, 3, CYCLE)
+                own_product(tile0 + 3, 0, HEADS - 1)
+                quantise_x(cycle + 1)
+                multiply_ab(duo0 + 2)
+                multiply_rope(tile0 + 4)
+                add(nc.vector, cycle, 2 * HEADS if ending else HEADS, 3 * HEADS)
+                store(tile0 + 2 if ending else tile0 + 1, tile0 + 3)
+                own_product(tile0 + 3, HEADS - 1, HEADS)
+                multiply_rope(tile0 + 5)
+                add(nc.gpsimd, cycle, 3 * HEADS, CYCLE * HEADS)
+                if cycle % CYCLES_PER_BATCH or ending:
+                    store(tile0 + 3, tile0 + 4)

@@ -21,6 +21,7 @@ BANK = 512
 PLANE = HEADS * PAIRS
 TILES_PER_BATCH = SEQ // P
 DUO = 2
+WARM_UP = 7
 CYCLE = 4
 CYCLES_PER_BATCH = TILES_PER_BATCH // CYCLE
 CYCLES = BATCH * CYCLES_PER_BATCH
@@ -233,8 +234,16 @@ def tile_multiheadlatentattention_pb_t_kernel(tc, x, cos, sin, wq, out):
                 in_=q_of[b][:, tiles, :, :].rearrange("p i h d -> p i (h d)"),
             )
 
+        def warm_up():
+            content_ps = psum.tile([P, BANK], F32)
+            for i in range(WARM_UP):
+                nc.tensor.matmul(
+                    out=content_ps[:], lhsT=x_sb[:, 0, 0, 0:P], rhs=x_sb[:, 0, 0, :], start=True, stop=True
+                )
+
         make_tables()
         transpose_x(0)
+        warm_up()
         regroup_x(0, 0)
         quantise_x(0, 0, 1)
         regroup_rope(1, lambda out, in_: nc.scalar.mul(out, in_, -1.0), 0, HEADS - 1)
@@ -313,10 +322,10 @@ def tile_multiheadlatentattention_pb_t_kernel(tc, x, cos, sin, wq, out):
                 quantise_x(cycle + 1)
                 multiply_ab(duo0 + 2)
                 multiply_rope(tile0 + 4)
-                add(nc.vector, cycle, 2 * HEADS if ending else HEADS, 3 * HEADS)
-                store(tile0 + 2 if ending else tile0 + 1, tile0 + 3)
                 own_product(tile0 + 3, HEADS - 1, HEADS)
                 multiply_rope(tile0 + 5)
+                add(nc.vector, cycle, 2 * HEADS if ending else HEADS, 3 * HEADS)
+                store(tile0 + 2 if ending else tile0 + 1, tile0 + 3)
                 add(nc.gpsimd, cycle, 3 * HEADS, CYCLE * HEADS)
                 if cycle % CYCLES_PER_BATCH or ending:
                     store(tile0 + 3, tile0 + 4)

@@ -21,10 +21,11 @@ BANK = 512
 PLANE = HEADS * PAIRS
 TILES_PER_BATCH = SEQ // P
 DUO = 2
-WARM_UP = 7
+WARM_UP = 6
 CYCLE = 4
 CYCLES_PER_BATCH = TILES_PER_BATCH // CYCLE
-CYCLES = BATCH * CYCLES_PER_BATCH
+CYCLES = BATCH * TILES_PER_BATCH // CYCLE
+DUOS = BATCH * TILES_PER_BATCH // DUO
 
 FLOPS = 2 * BATCH * SEQ * EMB * OUT_COLS
 
@@ -58,7 +59,7 @@ def tile_multiheadlatentattention_pb_t_kernel(tc, x, cos, sin, wq, out):
         identity = keep.tile([P, P], F32)
         make_identity(nc, identity[:])
 
-        x_words_of, grouped_of, x_mx_of = {}, {}, {}
+        x_words_of, x_split_of, grouped_of, x_mx_of = {}, {}, {}, {}
 
         def transpose_x(duo):
             x_words = psum.tile([P, DUO, 2, P], F32)
@@ -67,10 +68,25 @@ def tile_multiheadlatentattention_pb_t_kernel(tc, x, cos, sin, wq, out):
                 for u in range(2):
                     nc.tensor.transpose(
                         x_words[:, i, u, :],
-                        x_sb[:, b, t, :].bitcast(F32)[:, u : 2 * P : 2],
+                        x_split_of[duo][:, i, u, :]
+                        if duo in x_split_of
+                        else x_sb[:, b, t, :].bitcast(F32)[:, u : 2 * P : 2],
                         identity[:],
                     )
             x_words_of[duo] = x_words
+
+        def split_x(duo):
+            if 6 <= duo < DUOS and duo % 2 == 0:
+                b, t = divmod(DUO * duo, TILES_PER_BATCH)
+                x_split = stage.tile([P, DUO, 2, P], F32)
+                nc.scalar.copy(
+                    out=x_split[:],
+                    in_=x_sb[:, b, t : t + DUO, :]
+                    .rearrange("p i k -> p (i k)")
+                    .bitcast(F32)
+                    .rearrange("p (i w u) -> p i u w", i=DUO, u=2),
+                )
+                x_split_of[duo] = x_split
 
         def regroup_x(cycle, duo):
             if cycle not in grouped_of:
@@ -309,6 +325,8 @@ def tile_multiheadlatentattention_pb_t_kernel(tc, x, cos, sin, wq, out):
                 copy_content(tile)
             if not first:
                 transpose_ahead(cycle)
+            for duo in range(CYCLE // DUO * (cycle + 3), CYCLE // DUO * (cycle + 4)):
+                split_x(duo)
             if ending:
                 add(nc.vector, cycle, HEADS, 2 * HEADS)
                 store(tile0 + 1, tile0 + 2)
@@ -324,8 +342,12 @@ def tile_multiheadlatentattention_pb_t_kernel(tc, x, cos, sin, wq, out):
                 multiply_rope(tile0 + 4)
                 own_product(tile0 + 3, HEADS - 1, HEADS)
                 multiply_rope(tile0 + 5)
-                add(nc.vector, cycle, 2 * HEADS if ending else HEADS, 3 * HEADS)
-                store(tile0 + 2 if ending else tile0 + 1, tile0 + 3)
-                add(nc.gpsimd, cycle, 3 * HEADS, CYCLE * HEADS)
+                lh = 1 if cycle < 4 else 0
+                add(nc.vector, cycle, 2 * HEADS if ending else HEADS, 3 * HEADS - lh)
+                if not lh:
+                    store(tile0 + 2 if ending else tile0 + 1, tile0 + 3)
+                add(nc.gpsimd, cycle, 3 * HEADS - lh, CYCLE * HEADS)
+                if lh:
+                    store(tile0 + 1, tile0 + 3)
                 if cycle % CYCLES_PER_BATCH or ending:
                     store(tile0 + 3, tile0 + 4)

@@ -320,11 +320,12 @@ def tile_multiheadlatentattention_pb_t_kernel(tc, x, cos, sin, wq, out):
                 multiply_rope(tile0 + 3)
             shared_product(duo0 + 1)
             own_product(tile0 + 2)
-            for tile in range(tile0 + 2, tile0 + CYCLE):
-                multiply_content(tile)
-                copy_content(tile)
+            multiply_content(tile0 + 2)
+            copy_content(tile0 + 2)
             if not first:
                 transpose_ahead(cycle)
+            multiply_content(tile0 + 3)
+            copy_content(tile0 + 3)
             for duo in range(CYCLE // DUO * (cycle + 3), CYCLE // DUO * (cycle + 4)):
                 split_x(duo)
             if ending:

from contextlib import ExitStack

import concourse.mybir as mybir
from concourse.masks import make_identity

F32 = mybir.dt.float32
BF16 = mybir.dt.bfloat16
U32 = mybir.dt.uint32
U8 = mybir.dt.uint8
FP8X4 = mybir.dt.float8_e4m3fn_x4
ALU = mybir.AluOpType

P = 128
PACK = 4
BATCH, SEQ, EMB = 4, 1024, 512
HEADS, CONTENT, ROPE = 4, 128, 128
PAIRS = ROPE // 2
HEAD_COLS = CONTENT + ROPE
OUT_COLS = HEADS * HEAD_COLS
BANK = 512
PLANE = HEADS * PAIRS
TILES_PER_BATCH = SEQ // P
DUO = 2
WARM_UP = 6
CYCLE = 4
CYCLES_PER_BATCH = TILES_PER_BATCH // CYCLE
CYCLES = BATCH * TILES_PER_BATCH // CYCLE
DUOS = BATCH * TILES_PER_BATCH // DUO

FLOPS = 2 * BATCH * SEQ * EMB * OUT_COLS


def tile_multiheadlatentattention_pb_t_kernel(tc, x, cos, sin, wq, out):
    nc = tc.nc
    x_view = x.rearrange("b (p t) k -> p b t k", t=TILES_PER_BATCH)
    out_view = out.rearrange("b (p t) h d -> p b t (h d)", t=TILES_PER_BATCH)

    with ExitStack() as stack:
        keep = stack.enter_context(tc.tile_pool(name="keep", bufs=1))
        stage = stack.enter_context(tc.tile_pool(name="stage", bufs=5))
        products = stack.enter_context(tc.tile_pool(name="products", bufs=3))
        results = stack.enter_context(tc.tile_pool(name="results", bufs=3))
        psum = stack.enter_context(tc.psum_pool(name="psum", bufs=2))
        stack.enter_context(tc.manual_schedule())

        x_sb = keep.tile([P, BATCH, TILES_PER_BATCH, EMB], BF16)
        w_raw = keep.tile([P, PACK, OUT_COLS], BF16)
        cos_bf = keep.tile([P, TILES_PER_BATCH, PAIRS], BF16)
        sin_bf = keep.tile([P, TILES_PER_BATCH, PAIRS], BF16)
        nc.sync.dma_start(out=x_sb[:, 0, 0:DUO, :], in_=x_view[:, 0, 0:DUO, :])
        nc.sync.dma_start(out=cos_bf[:], in_=cos.rearrange("(p t) j -> p t j", t=TILES_PER_BATCH))
        nc.sync.dma_start(out=sin_bf[:], in_=sin.rearrange("(p t) j -> p t j", t=TILES_PER_BATCH))
        nc.sync.dma_start(out=w_raw[:], in_=wq.rearrange("(p t) c -> p t c", t=PACK))
        nc.sync.dma_start(out=x_sb[:, 0, DUO:CYCLE, :], in_=x_view[:, 0, DUO:CYCLE, :])
        nc.sync.dma_start(out=x_sb[:, 0, CYCLE:, :], in_=x_view[:, 0, CYCLE:, :])
        for b in range(1, BATCH):
            nc.sync.dma_start(out=x_sb[:, b, :, :], in_=x_view[:, b, :, :])

        identity = keep.tile([P, P], F32)
        make_identity(nc, identity[:])

        x_words_of, x_split_of, grouped_of, x_mx_of = {}, {}, {}, {}

        def transpose_x(duo):
            x_words = psum.tile([P, DUO, 2, P], F32)
            for i in range(DUO):
                b, t = divmod(DUO * duo + i, TILES_PER_BATCH)
                for u in range(2):
                    nc.tensor.transpose(
                        x_words[:, i, u, :],
                        x_split_of[duo][:, i, u, :]
                        if duo in x_split_of
                        else x_sb[:, b, t, :].bitcast(F32)[:, u : 2 * P : 2],
                        identity[:],
                    )
            x_words_of[duo] = x_words

        def split_x(duo):
            if 6 <= duo < DUOS and duo % 2 == 0:
                b, t = divmod(DUO * duo, TILES_PER_BATCH)
                x_split = stage.tile([P, DUO, 2, P], F32)
                nc.scalar.copy(
                    out=x_split[:],
                    in_=x_sb[:, b, t : t + DUO, :]
                    .rearrange("p i k -> p (i k)")
                    .bitcast(F32)
                    .rearrange("p (i w u) -> p i u w", i=DUO, u=2),
                )
                x_split_of[duo] = x_split

        def regroup_x(cycle, duo):
            if cycle not in grouped_of:
                x_grouped = stage.tile([P, CYCLE // DUO, DUO * P * PACK], BF16, align_bytes=64)
                grouped_of[cycle] = x_grouped
            nc.scalar.copy(
                out=grouped_of[cycle][:, duo, :]
                .bitcast(F32)
                .rearrange("p (i r u) -> p i r u", i=DUO, u=2),
                in_=x_words_of[CYCLE // DUO * cycle + duo][:].rearrange("p i u r -> p i r u"),
            )

        def quantise_x(cycle, duo0=0, duo1=CYCLE // DUO):
            if cycle not in x_mx_of:
                x_codes = stage.tile([P, CYCLE * P], U32, align_bytes=64)
                x_scales = stage.tile([P, CYCLE * P], U8, align_bytes=64)
                x_mx_of[cycle] = (x_codes, x_scales)
            x_codes, x_scales = x_mx_of[cycle]
            tokens = slice(duo0 * DUO * P, duo1 * DUO * P)
            nc.vector.quantize_mx(
                out=x_codes[:, tokens].bitcast(FP8X4),
                scales=x_scales[:, tokens],
                in_=grouped_of[cycle][:, duo0:duo1, :].rearrange("p i n -> p (i n)"),
            )

        w_grouped = keep.tile([P, OUT_COLS, PACK], BF16, align_bytes=64)
        w_codes = keep.tile([P, OUT_COLS], U32, align_bytes=64)
        w_scales = keep.tile([P, OUT_COLS], U8, align_bytes=64)
        content_cols = slice(0, BANK)
        rope_cols = slice(BANK, 2 * BANK)
        a_cols = slice(BANK, BANK + PLANE)
        b_cols = slice(BANK + PLANE, 2 * BANK)
        w_parts = w_raw[:].rearrange("p t (h x d) -> p t h x d", h=HEADS, x=2)
        w_rope = w_parts[:, :, :, 1, :].rearrange("p t h (j e) -> p t h j e", e=2)

        def regroup_content(copy, h0, h1):
            copy(
                out=w_grouped[:, h0 * CONTENT : h1 * CONTENT, :].rearrange(
                    "p (h d) t -> p h d t", d=CONTENT
                ),
                in_=w_parts[:, :, h0:h1, 0, :].rearrange("p t h d -> p h d t"),
            )

        def regroup_rope(e, copy, h0, h1):
            cols = (a_cols, b_cols)[e]
            copy(
                w_grouped[:, cols, :].rearrange("p (h j) t -> p h j t", h=HEADS)[:, h0:h1],
                w_rope[:, :, h0:h1, :, e].rearrange("p t h j -> p h j t"),
            )

        def quantise_w(c0, c1):
            nc.vector.quantize_mx(
                out=w_codes[:, c0:c1].bitcast(FP8X4),
                scales=w_scales[:, c0:c1],
                in_=w_grouped[:, c0:c1, :].rearrange("p c t -> p (c t)"),
            )

        sin_f = keep.tile([P, TILES_PER_BATCH, PAIRS], F32)
        mixed = keep.tile([P, TILES_PER_BATCH, 2, PAIRS], F32)

        def make_tables():
            nc.scalar.copy(out=sin_f[:], in_=sin_bf[:])
            nc.vector.tensor_tensor(
                out=mixed[:, :, 0, :], in0=cos_bf[:], in1=sin_bf[:], op=ALU.subtract
            )
            nc.vector.scalar_tensor_tensor(
                out=mixed[:, :, 1, :], in0=cos_bf[:], scalar=-1.0, in1=sin_bf[:],
                op0=ALU.mult, op1=ALU.subtract,
            )

        def multiply(sums, tile, cols, start, stop):
            cycle, i = divmod(tile, CYCLE)
            x_codes, x_scales = x_mx_of[cycle]
            tokens = slice(i * P, (i + 1) * P)
            nc.tensor.matmul_mx(
                out=sums,
                lhsT=x_codes[:, tokens].bitcast(FP8X4),
                lhsT_scale=x_scales[:, tokens],
                rhs=w_codes[:, cols].bitcast(FP8X4),
                rhs_scale=w_scales[:, cols],
                start=start,
                stop=stop,
            )

        ab_of, rope_of, content_of, cycle_of, q_of = {}, {}, {}, {}, {}

        def multiply_ab(duo):
            ab_ps = psum.tile([P, DUO, HEADS, PAIRS], F32)
            for i in range(DUO):
                group = ab_ps[:, i, :, :].rearrange("p h j -> p (h j)")
                multiply(group, DUO * duo + i, a_cols, True, False)
                multiply(group, DUO * duo + i, b_cols, False, True)
            ab_of[duo] = ab_ps

        def multiply_rope(tile):
            rope_ps = psum.tile([P, 2, HEADS, PAIRS], F32)
            multiply(rope_ps[:].rearrange("p e h j -> p (e h j)"), tile, rope_cols, True, True)
            rope_of[tile] = rope_ps

        def multiply_content(tile):
            content_ps = psum.tile([P, BANK], F32)
            multiply(content_ps[:], tile, content_cols, True, True)
            content_of[tile] = content_ps

        def open_cycle(cycle):
            shared = products.tile([P, CYCLE, HEADS, PAIRS], F32)
            own = products.tile([P, CYCLE, HEADS, PAIRS, 2], F32)
            batch, half = divmod(cycle, CYCLES_PER_BATCH)
            if half == 0:
                q_sb = results.tile([P, TILES_PER_BATCH, HEADS, HEAD_COLS], F32)
                q_of[batch] = q_sb
            cycle_of[cycle] = (shared, own, q_of[batch][:, half * CYCLE : (half + 1) * CYCLE, :, :])

        def shared_product(duo):
            cycle, i = divmod(DUO * duo, CYCLE)
            t0 = DUO * duo % TILES_PER_BATCH
            nc.vector.tensor_tensor(
                out=cycle_of[cycle][0][:, i : i + DUO, :, :],
                in0=ab_of[duo][:],
                in1=sin_f[:, t0 : t0 + DUO, :].unsqueeze(2).to_broadcast([P, DUO, HEADS, PAIRS]),
                op=ALU.mult,
            )

        def own_product(tile, h0=0, h1=HEADS):
            cycle, i = divmod(tile, CYCLE)
            nc.vector.tensor_tensor(
                out=cycle_of[cycle][1][:, i, h0:h1, :, :],
                in0=rope_of[tile][:, :, h0:h1, :].rearrange("p e h j -> p h j e"),
                in1=mixed[:, tile % TILES_PER_BATCH, :, :]
                .rearrange("p e j -> p j e")
                .unsqueeze(1)
                .to_broadcast([P, h1 - h0, PAIRS, 2]),
                op=ALU.mult,
            )

        def copy_content(tile):
            cycle, i = divmod(tile, CYCLE)
            nc.scalar.copy(
                out=cycle_of[cycle][2][:, i, :, 0:CONTENT],
                in_=content_of[tile][:].rearrange("p (h d) -> p h d", h=HEADS),
            )

        def add(engine, cycle, n0, n1):
            shared, own, q_sb = cycle_of[cycle]
            engine.tensor_tensor(
                out=q_sb.rearrange("p i h d -> p (i h) d")[:, n0:n1, CONTENT:]
                .rearrange("p n (j e) -> p n j e", e=2),
                in0=shared[:]
                .rearrange("p i h j -> p (i h) j")[:, n0:n1, :]
                .unsqueeze(3)
                .to_broadcast([P, n1 - n0, PAIRS, 2]),
                in1=own[:].rearrange("p i h j e -> p (i h) j e")[:, n0:n1, :, :],
                op=ALU.add,
            )

        def store(tile0, tile1):
            b, t0 = divmod(tile0, TILES_PER_BATCH)
            tiles = slice(t0, t0 + tile1 - tile0)
            nc.sync.dma_start(
                out=out_view[:, b, tiles, :],
                in_=q_of[b][:, tiles, :, :].rearrange("p i h d -> p i (h d)"),
            )

        def warm_up():
            content_ps = psum.tile([P, BANK], F32)
            for i in range(WARM_UP):
                nc.tensor.matmul(
                    out=content_ps[:], lhsT=x_sb[:, 0, 0, 0:P], rhs=x_sb[:, 0, 0, :], start=True, stop=True
                )

        make_tables()
        transpose_x(0)
        warm_up()
        regroup_x(0, 0)
        quantise_x(0, 0, 1)
        regroup_rope(1, lambda out, in_: nc.scalar.mul(out, in_, -1.0), 0, HEADS - 1)
        regroup_rope(0, nc.vector.tensor_copy, 0, HEADS)
        regroup_rope(1, lambda out, in_: nc.vector.tensor_scalar_mul(out, in_, -1.0), HEADS - 1, HEADS)
        transpose_x(1)
        regroup_x(0, 1)
        quantise_w(BANK, BANK + PLANE)
        quantise_w(BANK + PLANE, 2 * BANK)
        regroup_content(nc.vector.tensor_copy, 0, 2)
        regroup_content(nc.scalar.copy, 2, 4)
        open_cycle(0)
        multiply_rope(0)
        multiply_rope(1)
        own_product(0)
        own_product(1)
        for duo in range(CYCLE // DUO):
            transpose_x(CYCLE // DUO + duo)
            regroup_x(1, duo)
        multiply_ab(0)
        quantise_x(0, 1, 2)
        quantise_w(0, BANK)
        shared_product(0)
        multiply_ab(1)
        multiply_rope(2)
        multiply_rope(3)

        def transpose_ahead(cycle):
            if cycle + 2 < CYCLES:
                for duo in range(CYCLE // DUO):
                    transpose_x(CYCLE // DUO * (cycle + 2) + duo)
                    regroup_x(cycle + 2, duo)

        for cycle in range(CYCLES):
            first, last = cycle == 0, cycle == CYCLES - 1
            ending = cycle >= CYCLES - CYCLES_PER_BATCH
            tile0, duo0 = CYCLE * cycle, CYCLE // DUO * cycle
            if not first:
                open_cycle(cycle)
                shared_product(duo0)
                own_product(tile0)
                multiply_ab(duo0 + 1)
            multiply_content(tile0)
            copy_content(tile0)
            add(nc.gpsimd, cycle, 0, HEADS)
            if cycle % CYCLES_PER_BATCH and not ending:
                store(tile0 - 1, tile0 + 1)
            else:
                store(tile0, tile0 + 1)
            if not first:
                own_product(tile0 + 1)
            multiply_content(tile0 + 1)
            copy_content(tile0 + 1)
            if first:
                transpose_ahead(cycle)
            else:
                multiply_rope(tile0 + 2)
                multiply_rope(tile0 + 3)
            shared_product(duo0 + 1)
            own_product(tile0 + 2)
            multiply_content(tile0 + 2)
            copy_content(tile0 + 2)
            if not first:
                transpose_ahead(cycle)
            multiply_content(tile0 + 3)
            copy_content(tile0 + 3)
            for duo in range(CYCLE // DUO * (cycle + 3), CYCLE // DUO * (cycle + 4)):
                split_x(duo)
            if ending:
                add(nc.vector, cycle, HEADS, 2 * HEADS)
                store(tile0 + 1, tile0 + 2)
            if last:
                own_product(tile0 + 3)
                for n in (2, 3):
                    add(nc.vector, cycle, n * HEADS, (n + 1) * HEADS)
                    store(tile0 + n, tile0 + n + 1)
            else:
                own_product(tile0 + 3, 0, HEADS - 1)
                quantise_x(cycle + 1)
                multiply_ab(duo0 + 2)
                multiply_rope(tile0 + 4)
                own_product(tile0 + 3, HEADS - 1, HEADS)
                multiply_rope(tile0 + 5)
                lh = 1 if cycle < 4 else 0
                add(nc.vector, cycle, 2 * HEADS if ending else HEADS, 3 * HEADS - lh)
                if not lh:
                    store(tile0 + 2 if ending else tile0 + 1, tile0 + 3)
                add(nc.gpsimd, cycle, 3 * HEADS - lh, CYCLE * HEADS)
                if lh:
                    store(tile0 + 1, tile0 + 3)
                if cycle % CYCLES_PER_BATCH or ending:
                    store(tile0 + 3, tile0 + 4)
